import numpy as np
import ml_dtypes


def mxq(x, axis, fmt="e4m3"):
    dtype, down = {"e4m3": (ml_dtypes.float8_e4m3fn, 7), "e5m2": (ml_dtypes.float8_e5m2, 14)}[fmt]
    v = np.moveaxis(np.asarray(x, np.float32).astype(ml_dtypes.bfloat16).astype(np.float64), axis, -1)
    blocks = v.reshape(v.shape[:-1] + (-1, 32))
    amax = np.abs(blocks).max(-1, keepdims=True)
    byte = np.maximum(np.where(amax > 0, np.frexp(amax)[1] - 1 + 127, 0) - down, 1)
    scale = np.exp2(byte - 127.0)
    codes = (blocks / scale).astype(np.float32).astype(dtype).astype(np.float64)
    return np.moveaxis((codes * scale).reshape(v.shape), -1, axis)


WIDE = False


def mx_kscale(k):
    if not WIDE:
        return np.ones(k)
    levels = np.array([10, -10, 5, -5, 0])
    a = np.random.permutation(np.resize(levels, k // 512 * 4)).reshape(k // 512, 4)
    idx = np.arange(k)
    return np.exp2(a[idx // 512, idx % 128 // 32])


BF16 = ml_dtypes.bfloat16


def bf(x):
    return np.asarray(x, np.float32).astype(BF16)


def f64(x):
    return np.asarray(x).astype(np.float64)


B, In, H, Hh, E, G = 512, 1024, 1024, 256, 128, 4
EPS = 1e-6


def rn(*shape):
    return np.random.standard_normal(shape)


def sigmoid(v):
    return 1.0 / (1.0 + np.exp(-v))


def ln(a, gamma, beta):
    mean = a.mean(-1, keepdims=True)
    std = a.std(-1, keepdims=True, ddof=1)
    return gamma * (a - mean) / (std + EPS) + beta


def expand(emb, w):
    return (emb.transpose(1, 0, 2) @ w.transpose(0, 2, 1)).transpose(1, 0, 2)


def setup_inputs():
    s, t = mx_kscale(In), mx_kscale(H)
    return {
        'x': bf(rn(B, In) * s),
        'h': bf(rn(B, H) * t),
        'c': bf(rn(B, H)),
        'emb_h': bf(1.0 + 0.5 * rn(B, G, E)),
        'emb_x': bf(1.0 + 0.5 * rn(B, G, E)),
        'emb_b': bf(rn(B, G, E)),
        'Wsh': bf(1.0 / E + 0.5 * rn(G, H, E) / np.sqrt(E)),
        'Wsx': bf(1.0 / E + 0.5 * rn(G, H, E) / np.sqrt(E)),
        'Wsb': bf(0.5 * rn(G, H, E) / np.sqrt(E)),
        'Wih': bf(rn(G * H, In) / np.sqrt(In) / s[None, :]),
        'Whh': bf(rn(G * H, H) / np.sqrt(H) / t[None, :]),
        'bias': bf(0.3 * rn(G * H)),
        'ln_gamma': bf(1.0 + 0.1 * rn(G, H)),
        'ln_beta': bf(0.1 * rn(G, H)),
        'lnc_gamma': bf(1.0 + 0.1 * rn(H)),
        'lnc_beta': bf(0.1 * rn(H)),
    }


def reference(x, h, c, emb_h, emb_x, emb_b, Wsh, Wsx, Wsb, Wih, Whh, bias, ln_gamma, ln_beta, lnc_gamma, lnc_beta):
    zh = expand(f64(emb_h), f64(Wsh))
    zx = expand(f64(emb_x), f64(Wsx))
    zb = expand(f64(emb_b), f64(Wsb))
    xh = (mxq(f64(x), 1, 'e4m3') @ mxq(f64(Wih).T, 0, 'e4m3')).reshape(B, G, H)
    hh = (mxq(f64(h), 1, 'e4m3') @ mxq(f64(Whh).T, 0, 'e4m3')).reshape(B, G, H)
    gates = xh * zx + hh * zh + (f64(bias).reshape(G, H) + zb)
    gates = ln(gates, f64(ln_gamma), f64(ln_beta))
    i, f, g, o = gates[:, 0], gates[:, 1], gates[:, 2], gates[:, 3]
    new_c = f64(c) * sigmoid(f) + sigmoid(i) * np.tanh(g)
    new_c = ln(new_c, f64(lnc_gamma), f64(lnc_beta))
    new_h = np.tanh(new_c) * sigmoid(o)
    return new_h, new_c

@@ -1,0 +1,261 @@
+import math
+from contextlib import ExitStack
+
+import concourse.mybir as mybir
+from concourse.masks import make_identity
+
+F32 = mybir.dt.float32
+BF16 = mybir.dt.bfloat16
+U32 = mybir.dt.uint32
+U8 = mybir.dt.uint8
+FP8X4 = mybir.dt.float8_e4m3fn_x4
+ACT = mybir.ActivationFunctionType
+ALU = mybir.AluOpType
+AXIS = mybir.AxisListType
+
+P = 128
+B = 512
+K = 1024
+H = 1024
+E = 128
+GATES = 4
+BATCH_TILES = B // P
+K_PASS = 4 * P
+PASSES = K // K_PASS
+ROWS = 512
+HALVES = H // ROWS
+STEPS = BATCH_TILES * HALVES
+EPS = 1e-6
+
+GATE_I, GATE_F, GATE_G, GATE_O = 0, 1, 2, 3
+GATE_ORDER = (GATE_I, GATE_G, GATE_F, GATE_O)
+
+FLOPS = 2 * (2 * B * K * GATES * H) + 3 * (2 * B * E * GATES * H)
+
+
+def tile_hyperlstmcell_pb_kernel(
+    tc, x, h, c, emb_h, emb_x, emb_b, Wsh, Wsx, Wsb, Wih, Whh, bias,
+    ln_gamma, ln_beta, lnc_gamma, lnc_beta, out_0, out_1,
+):
+    nc = tc.nc
+    big_weight = {"x": Wih, "h": Whh}
+    small_weight = {"x": Wsx, "h": Wsh, "b": Wsb}
+    embedding = {"x": emb_x, "h": emb_h, "b": emb_b}
+
+    with ExitStack() as ctx:
+        const = ctx.enter_context(tc.tile_pool(name="const", bufs=1))
+        keep = ctx.enter_context(tc.tile_pool(name="keep", bufs=1))
+        big_rows = ctx.enter_context(tc.tile_pool(name="big_rows", bufs=3))
+        small_rows = ctx.enter_context(tc.tile_pool(name="small_rows", bufs=3))
+        grouped_pool = ctx.enter_context(tc.tile_pool(name="grouped", bufs=3))
+        per_gate = ctx.enter_context(tc.tile_pool(name="per_gate", bufs=2))
+        work = ctx.enter_context(tc.tile_pool(name="work", bufs=3))
+        pre_pool = ctx.enter_context(tc.tile_pool(name="pre", bufs=4))
+        scratch = ctx.enter_context(tc.tile_pool(name="scratch", bufs=2))
+        results = ctx.enter_context(tc.tile_pool(name="results", bufs=2))
+        stats = ctx.enter_context(tc.tile_pool(name="stats", bufs=4))
+        psum_words = ctx.enter_context(tc.psum_pool(name="psum_words", bufs=2))
+        psum_small = ctx.enter_context(tc.psum_pool(name="psum_small", bufs=1))
+        psum_out = ctx.enter_context(tc.psum_pool(name="psum_out", bufs=1))
+
+        ident_f32 = const.tile([P, P], F32)
+        make_identity(nc, ident_f32[:])
+        ident_bf16 = const.tile([P, P], BF16)
+        make_identity(nc, ident_bf16[:])
+        exp_half = const.tile([P, 1], F32)
+        nc.vector.memset(exp_half[:], 0.5)
+
+        def load_rows(dram_rows):
+            rows_sb = big_rows.tile([P, ROWS // P, K], BF16)
+            nc.sync.dma_start(out=rows_sb[:], in_=dram_rows.rearrange("(r p) k -> p r k", p=P))
+            return rows_sb
+
+        def quantise_pass(rows_sb, g, codes, scales):
+            grouped = grouped_pool.tile([P, 4 * ROWS], BF16, align_bytes=64)
+            grouped_words = grouped[:].bitcast(F32).rearrange("p (r u) -> p r u", u=2)
+            for pair in range(2):
+                bank = psum_words.tile([P, 2, 2 * P], F32)
+                for u in range(2):
+                    for r in range(2):
+                        first_word = 2 * P * g + P * u
+                        nc.tensor.transpose(
+                            bank[:, u, r * P : (r + 1) * P],
+                            rows_sb[:, 2 * pair + r, :].bitcast(F32)[:, first_word : first_word + P],
+                            ident_f32[:],
+                        )
+                nc.scalar.copy(
+                    out=grouped_words[:, 2 * P * pair : 2 * P * (pair + 1), :],
+                    in_=bank[:].rearrange("p u r -> p r u"),
+                )
+            nc.vector.quantize_mx(out=codes.bitcast(FP8X4), scales=scales, in_=grouped[:])
+
+        def transpose_eight(blocks, dst):
+            bank = psum_small.tile([P, 8 * P], BF16)
+            for i, block in enumerate(blocks):
+                nc.tensor.transpose(bank[:, i * P : (i + 1) * P], block, ident_bf16[:])
+            nc.scalar.copy(out=dst, in_=bank[:])
+
+        def prepare(gate, step, parts):
+            if step == 0:
+                for name in ("x", "h"):
+                    parts["codes_" + name] = per_gate.tile([P, PASSES, H], U32, align_bytes=64, name="codes_" + name)
+                    parts["scales_" + name] = per_gate.tile([P, PASSES, H], U8, align_bytes=64, name="scales_" + name)
+            half, name, g = step // 4, ("x", "h")[(step // 2) % 2], step % 2
+            units = slice(half * ROWS, (half + 1) * ROWS)
+            if g == 0:
+                first_row = gate * H + half * ROWS
+                parts["rows"] = load_rows(big_weight[name][first_row : first_row + ROWS, :])
+            quantise_pass(parts["rows"], g, parts["codes_" + name][:, g, units], parts["scales_" + name][:, g, units])
+            if step < 3:
+                name = ("x", "h", "b")[step]
+                w_rows = small_rows.tile([P, H // P, E], BF16, tag="rows")
+                nc.sync.dma_start(out=w_rows[:], in_=small_weight[name][gate].rearrange("(j p) e -> p j e", p=P))
+                small_t = per_gate.tile([P, H], BF16, name="small_" + name)
+                transpose_eight([w_rows[:, j, :] for j in range(H // P)], small_t[:])
+                parts["small_" + name] = small_t
+            if step == 3:
+                for name, vector in (
+                    ("bias", bias[gate * H : (gate + 1) * H]), ("gain", ln_gamma[gate, :]), ("shift", ln_beta[gate, :]),
+                ):
+                    parts[name] = per_gate.tile([P, H], BF16, name=name)
+                    nc.sync.dma_start(out=parts[name][:], in_=vector.partition_broadcast(P))
+
+        def output_tile(gate, m, half, parts, pre, sums):
+            samples = slice(m * P, (m + 1) * P)
+            units = slice(half * ROWS, (half + 1) * ROWS)
+            z = {}
+            for name in ("x", "h", "b"):
+                z[name] = psum_out.tile([P, ROWS], F32, name="z_" + name)
+                nc.tensor.matmul(
+                    out=z[name][:], lhsT=emb_t[name][:, gate, samples], rhs=parts["small_" + name][:, units],
+                    start=True, stop=True,
+                )
+            term = {}
+            for i, name in enumerate(("x", "h")):
+                product = psum_out.tile([P, ROWS], F32, name="product_" + name)
+                for g in range(PASSES):
+                    nc.tensor.matmul_mx(
+                        out=product[:],
+                        lhsT=act_codes[name][:, g, samples].bitcast(FP8X4),
+                        lhsT_scale=act_scales[name][:, g, samples],
+                        rhs=parts["codes_" + name][:, g, units].bitcast(FP8X4),
+                        rhs_scale=parts["scales_" + name][:, g, units],
+                        start=(g == 0),
+                        stop=(g == PASSES - 1),
+                    )
+                z_sb = work.tile([P, ROWS], F32, name="z_sb_" + name)
+                nc.scalar.copy(out=z_sb[:], in_=z[name][:])
+                term[name] = work.tile([P, ROWS], F32, name="term_" + name)
+                nc.vector.scalar_tensor_tensor(
+                    out=term[name][:], in0=product[:], scalar=1.0, in1=z_sb[:], op0=ALU.mult, op1=ALU.mult,
+                    accum_out=sums[:, 3 * half + i : 3 * half + i + 1],
+                )
+            term["b"] = work.tile([P, ROWS], F32, name="term_b")
+            nc.vector.scalar_tensor_tensor(
+                out=term["b"][:], in0=z["b"][:], scalar=1.0, in1=parts["bias"][:, units], op0=ALU.mult, op1=ALU.add,
+                accum_out=sums[:, 3 * half + 2 : 3 * half + 3],
+            )
+            nc.gpsimd.tensor_tensor(out=term["x"][:], in0=term["x"][:], in1=term["h"][:], op=ALU.add)
+            nc.gpsimd.tensor_tensor(out=pre[:, units], in0=term["x"][:], in1=term["b"][:], op=ALU.add)
+
+        def row_stats(values, sums):
+            total = stats.tile([P, 1], F32)
+            nc.vector.tensor_reduce(out=total[:], in_=sums, axis=AXIS.X, op=ALU.add)
+            neg_mean = stats.tile([P, 1], F32)
+            nc.vector.tensor_scalar_mul(out=neg_mean[:], in0=total[:], scalar1=-1.0 / H)
+            squares = scratch.tile([P, H], BF16)
+            sum_sq = stats.tile([P, 1], F32)
+            nc.scalar.activation(
+                out=squares[:], in_=values, func=ACT.Square, bias=neg_mean[:, 0:1], scale=1.0, accum_out=sum_sq[:],
+            )
+            root = stats.tile([P, 1], F32)
+            nc.gpsimd.tensor_tensor(out=root[:], in0=sum_sq[:], in1=exp_half[:], op=ALU.pow)
+            std_eps = stats.tile([P, 1], F32)
+            nc.vector.tensor_scalar(
+                out=std_eps[:], in0=root[:], scalar1=1.0 / math.sqrt(H - 1), scalar2=EPS, op0=ALU.mult, op1=ALU.add,
+            )
+            inv_std = stats.tile([P, 1], F32)
+            nc.vector.reciprocal(out=inv_std[:], in_=std_eps[:])
+            return neg_mean, inv_std
+
+        def normalise(out, values, neg_mean, inv_std, gain, shift):
+            nc.vector.scalar_tensor_tensor(
+                out=out, in0=values, scalar=neg_mean[:, 0:1], in1=gain, op0=ALU.add, op1=ALU.mult,
+            )
+            nc.vector.scalar_tensor_tensor(
+                out=out, in0=out, scalar=inv_std[:, 0:1], in1=shift, op0=ALU.mult, op1=ALU.add,
+            )
+
+        def finish_gate(gate, m, parts, pre, sums):
+            cell_m = cell[:, m, :]
+            neg_mean, inv_std = row_stats(pre[:], sums[:])
+            normalise(pre[:], pre[:], neg_mean, inv_std, parts["gain"][:], parts["shift"][:])
+            if gate == GATE_I:
+                nc.scalar.activation(out=cell_m, in_=pre[:], func=ACT.Sigmoid)
+            elif gate == GATE_G:
+                nc.scalar.activation(out=pre[:], in_=pre[:], func=ACT.Tanh)
+                nc.vector.tensor_tensor(out=cell_m, in0=cell_m, in1=pre[:], op=ALU.mult)
+            elif gate == GATE_F:
+                nc.scalar.activation(out=pre[:], in_=pre[:], func=ACT.Sigmoid)
+                nc.vector.tensor_tensor(out=pre[:], in0=pre[:], in1=c_sb[:, m, :], op=ALU.mult)
+                cell_sum = stats.tile([P, 1], F32)
+                nc.vector.scalar_tensor_tensor(
+                    out=cell_m, in0=pre[:], scalar=1.0, in1=cell_m, op0=ALU.mult, op1=ALU.add, accum_out=cell_sum[:],
+                )
+                neg_mean, inv_std = row_stats(cell_m, cell_sum[:])
+                new_c = results.tile([P, H], F32, tag="result")
+                normalise(new_c[:], cell_m, neg_mean, inv_std, cell_gain[:], cell_shift[:])
+                nc.sync.dma_start(out=out_1[m * P : (m + 1) * P, :], in_=new_c[:])
+                nc.scalar.activation(out=cell_m, in_=new_c[:], func=ACT.Tanh)
+            else:
+                nc.scalar.activation(out=pre[:], in_=pre[:], func=ACT.Sigmoid)
+                new_h = results.tile([P, H], F32, tag="result")
+                nc.vector.tensor_tensor(out=new_h[:], in0=pre[:], in1=cell_m, op=ALU.mult)
+                nc.sync.dma_start(out=out_0[m * P : (m + 1) * P, :], in_=new_h[:])
+
+        act_codes, act_scales = {}, {}
+        for name, activations in (("x", x), ("h", h)):
+            act_codes[name] = keep.tile([P, PASSES, B], U32, align_bytes=64, name="act_codes_" + name)
+            act_scales[name] = keep.tile([P, PASSES, B], U8, align_bytes=64, name="act_scales_" + name)
+            rows_sb = load_rows(activations)
+            for g in range(PASSES):
+                quantise_pass(rows_sb, g, act_codes[name][:, g, :], act_scales[name][:, g, :])
+
+        emb_t = {}
+        for name in ("x", "h", "b"):
+            emb_rows = small_rows.tile([P, BATCH_TILES, GATES * E], BF16, tag="rows")
+            nc.sync.dma_start(out=emb_rows[:], in_=embedding[name].rearrange("(m p) g e -> p m (g e)", p=P))
+            emb_t[name] = keep.tile([P, GATES, B], BF16, name="emb_t_" + name)
+            for first_gate in range(0, GATES, 2):
+                transpose_eight(
+                    [
+                        emb_rows[:, m, gate * E : (gate + 1) * E]
+                        for gate in (first_gate, first_gate + 1)
+                        for m in range(BATCH_TILES)
+                    ],
+                    emb_t[name][:, first_gate : first_gate + 2, :].rearrange("p g b -> p (g b)"),
+                )
+
+        parts = {}
+        for step in range(STEPS):
+            prepare(GATE_ORDER[0], step, parts)
+
+        c_sb = keep.tile([P, BATCH_TILES, H], BF16)
+        nc.sync.dma_start(out=c_sb[:], in_=c.rearrange("(m p) n -> p m n", p=P))
+        cell_gain = keep.tile([P, H], BF16)
+        nc.sync.dma_start(out=cell_gain[:], in_=lnc_gamma.partition_broadcast(P))
+        cell_shift = keep.tile([P, H], BF16)
+        nc.sync.dma_start(out=cell_shift[:], in_=lnc_beta.partition_broadcast(P))
+        cell = keep.tile([P, BATCH_TILES, H], F32)
+
+        for position, gate in enumerate(GATE_ORDER):
+            next_parts = {}
+            for m in range(BATCH_TILES):
+                pre = pre_pool.tile([P, H], F32)
+                sums = stats.tile([P, 3 * HALVES], F32)
+                for half in range(HALVES):
+                    output_tile(gate, m, half, parts, pre, sums)
+                    if position + 1 < GATES:
+                        prepare(GATE_ORDER[position + 1], m * HALVES + half, next_parts)
+                finish_gate(gate, m, parts, pre, sums)
+            parts = next_parts

@@ -155,8 +155,8 @@ def tile_hyperlstmcell_pb_kernel(
                 out=term["b"][:], in0=z["b"][:], scalar=1.0, in1=parts["bias"][:, units], op0=ALU.mult, op1=ALU.add,
                 accum_out=sums[:, 3 * half + 2 : 3 * half + 3],
             )
-            nc.gpsimd.tensor_tensor(out=term["x"][:], in0=term["x"][:], in1=term["h"][:], op=ALU.add)
-            nc.gpsimd.tensor_tensor(out=pre[:, units], in0=term["x"][:], in1=term["b"][:], op=ALU.add)
+            nc.vector.tensor_tensor(out=term["x"][:], in0=term["x"][:], in1=term["h"][:], op=ALU.add)
+            nc.vector.tensor_tensor(out=pre[:, units], in0=term["x"][:], in1=term["b"][:], op=ALU.add)
 
         def row_stats(values, sums):
             total = stats.tile([P, 1], F32)

@@ -11,7 +11,6 @@ U8 = mybir.dt.uint8
 FP8X4 = mybir.dt.float8_e4m3fn_x4
 ACT = mybir.ActivationFunctionType
 ALU = mybir.AluOpType
-AXIS = mybir.AxisListType
 
 P = 128
 B = 512
@@ -24,13 +23,31 @@ K_PASS = 4 * P
 PASSES = K // K_PASS
 ROWS = 512
 HALVES = H // ROWS
-STEPS = BATCH_TILES * HALVES
+TILES_PER_GATE = HALVES * BATCH_TILES
+N_TILES = GATES * TILES_PER_GATE
 EPS = 1e-6
 
 GATE_I, GATE_F, GATE_G, GATE_O = 0, 1, 2, 3
 GATE_ORDER = (GATE_I, GATE_G, GATE_F, GATE_O)
 
+STEPS_PER_HALF_GATE = 2 * PASSES
+N_STEPS = GATES * HALVES * STEPS_PER_HALF_GATE
+QUANTISE_AHEAD = STEPS_PER_HALF_GATE + 1
+TURN_AHEAD = QUANTISE_AHEAD + 1
+LOAD_AHEAD = 6
+LAST_LAG = 3
+
 FLOPS = 2 * (2 * B * K * GATES * H) + 3 * (2 * B * E * GATES * H)
+
+
+def where(t):
+    return t // TILES_PER_GATE, (t % TILES_PER_GATE) // BATCH_TILES, t % BATCH_TILES
+
+
+def completed_row(t):
+    if 0 <= t < N_TILES and where(t)[1] == HALVES - 1:
+        return where(t)[0], where(t)[2]
+    return None
 
 
 def tile_hyperlstmcell_pb_kernel(
@@ -45,18 +62,22 @@ def tile_hyperlstmcell_pb_kernel(
     with ExitStack() as ctx:
         const = ctx.enter_context(tc.tile_pool(name="const", bufs=1))
         keep = ctx.enter_context(tc.tile_pool(name="keep", bufs=1))
-        big_rows = ctx.enter_context(tc.tile_pool(name="big_rows", bufs=3))
+        big_rows = ctx.enter_context(tc.tile_pool(name="big_rows", bufs=4))
         small_rows = ctx.enter_context(tc.tile_pool(name="small_rows", bufs=3))
         grouped_pool = ctx.enter_context(tc.tile_pool(name="grouped", bufs=3))
+        half_gate = ctx.enter_context(tc.tile_pool(name="half_gate", bufs=2))
         per_gate = ctx.enter_context(tc.tile_pool(name="per_gate", bufs=2))
-        work = ctx.enter_context(tc.tile_pool(name="work", bufs=3))
-        pre_pool = ctx.enter_context(tc.tile_pool(name="pre", bufs=4))
+        work = ctx.enter_context(tc.tile_pool(name="work", bufs=2))
+        z_pool = ctx.enter_context(tc.tile_pool(name="z_sb", bufs=3))
+        pre_pool = ctx.enter_context(tc.tile_pool(name="pre", bufs=5))
+        sums_pool = ctx.enter_context(tc.tile_pool(name="sums", bufs=6))
+        scaled_pool = ctx.enter_context(tc.tile_pool(name="scaled", bufs=3))
         scratch = ctx.enter_context(tc.tile_pool(name="scratch", bufs=2))
         results = ctx.enter_context(tc.tile_pool(name="results", bufs=2))
         stats = ctx.enter_context(tc.tile_pool(name="stats", bufs=4))
-        psum_words = ctx.enter_context(tc.psum_pool(name="psum_words", bufs=2))
-        psum_small = ctx.enter_context(tc.psum_pool(name="psum_small", bufs=1))
         psum_out = ctx.enter_context(tc.psum_pool(name="psum_out", bufs=1))
+        psum_turn = ctx.enter_context(tc.psum_pool(name="psum_turn", bufs=3))
+        ctx.enter_context(tc.manual_schedule())
 
         ident_f32 = const.tile([P, P], F32)
         make_identity(nc, ident_f32[:])
@@ -64,17 +85,19 @@ def tile_hyperlstmcell_pb_kernel(
         make_identity(nc, ident_bf16[:])
         exp_half = const.tile([P, 1], F32)
         nc.vector.memset(exp_half[:], 0.5)
+        exp_minus_one = const.tile([P, 1], F32)
+        nc.vector.memset(exp_minus_one[:], -1.0)
 
         def load_rows(dram_rows):
             rows_sb = big_rows.tile([P, ROWS // P, K], BF16)
             nc.sync.dma_start(out=rows_sb[:], in_=dram_rows.rearrange("(r p) k -> p r k", p=P))
             return rows_sb
 
-        def quantise_pass(rows_sb, g, codes, scales):
+        def turn(rows_sb, g, vector_helps):
             grouped = grouped_pool.tile([P, 4 * ROWS], BF16, align_bytes=64)
             grouped_words = grouped[:].bitcast(F32).rearrange("p (r u) -> p r u", u=2)
             for pair in range(2):
-                bank = psum_words.tile([P, 2, 2 * P], F32)
+                bank = psum_turn.tile([P, 2, 2 * P], F32, tag="turned")
                 for u in range(2):
                     for r in range(2):
                         first_word = 2 * P * g + P * u
@@ -83,86 +106,107 @@ def tile_hyperlstmcell_pb_kernel(
                             rows_sb[:, 2 * pair + r, :].bitcast(F32)[:, first_word : first_word + P],
                             ident_f32[:],
                         )
-                nc.scalar.copy(
-                    out=grouped_words[:, 2 * P * pair : 2 * P * (pair + 1), :],
-                    in_=bank[:].rearrange("p u r -> p r u"),
-                )
+                target = grouped_words[:, 2 * P * pair : 2 * P * (pair + 1), :]
+                if vector_helps and pair == 1:
+                    nc.vector.tensor_copy(out=target, in_=bank[:].rearrange("p u r -> p r u"))
+                else:
+                    nc.scalar.copy(out=target, in_=bank[:].rearrange("p u r -> p r u"))
+            return grouped
+
+        def quantise(grouped, codes, scales):
             nc.vector.quantize_mx(out=codes.bitcast(FP8X4), scales=scales, in_=grouped[:])
 
         def transpose_eight(blocks, dst):
-            bank = psum_small.tile([P, 8 * P], BF16)
+            bank = psum_turn.tile([P, 8 * P], BF16, tag="turned")
             for i, block in enumerate(blocks):
                 nc.tensor.transpose(bank[:, i * P : (i + 1) * P], block, ident_bf16[:])
             nc.scalar.copy(out=dst, in_=bank[:])
 
-        def prepare(gate, step, parts):
-            if step == 0:
-                for name in ("x", "h"):
-                    parts["codes_" + name] = per_gate.tile([P, PASSES, H], U32, align_bytes=64, name="codes_" + name)
-                    parts["scales_" + name] = per_gate.tile([P, PASSES, H], U8, align_bytes=64, name="scales_" + name)
-            half, name, g = step // 4, ("x", "h")[(step // 2) % 2], step % 2
-            units = slice(half * ROWS, (half + 1) * ROWS)
-            if g == 0:
-                first_row = gate * H + half * ROWS
-                parts["rows"] = load_rows(big_weight[name][first_row : first_row + ROWS, :])
-            quantise_pass(parts["rows"], g, parts["codes_" + name][:, g, units], parts["scales_" + name][:, g, units])
-            if step < 3:
-                name = ("x", "h", "b")[step]
-                w_rows = small_rows.tile([P, H // P, E], BF16, tag="rows")
-                nc.sync.dma_start(out=w_rows[:], in_=small_weight[name][gate].rearrange("(j p) e -> p j e", p=P))
-                small_t = per_gate.tile([P, H], BF16, name="small_" + name)
-                transpose_eight([w_rows[:, j, :] for j in range(H // P)], small_t[:])
-                parts["small_" + name] = small_t
-            if step == 3:
-                for name, vector in (
-                    ("bias", bias[gate * H : (gate + 1) * H]), ("gain", ln_gamma[gate, :]), ("shift", ln_beta[gate, :]),
-                ):
-                    parts[name] = per_gate.tile([P, H], BF16, name=name)
-                    nc.sync.dma_start(out=parts[name][:], in_=vector.partition_broadcast(P))
+        def load_gate_vectors(position, parts):
+            gate = GATE_ORDER[position]
+            for name, vector in (
+                ("bias", bias[gate * H : (gate + 1) * H]), ("gain", ln_gamma[gate, :]), ("shift", ln_beta[gate, :]),
+            ):
+                parts[name] = per_gate.tile([P, H], BF16, name=name)
+                nc.gpsimd.dma_start(out=parts[name][:], in_=vector.partition_broadcast(P))
 
-        def output_tile(gate, m, half, parts, pre, sums):
+        def load_small_weights(position, parts):
+            gate = GATE_ORDER[position]
+            for name in ("x", "h", "b"):
+                parts["rows_" + name] = small_rows.tile([P, H // P, E], BF16, name="rows_" + name, tag="rows")
+                nc.sync.dma_start(
+                    out=parts["rows_" + name][:], in_=small_weight[name][gate].rearrange("(j p) e -> p j e", p=P)
+                )
+
+        def turn_small_weight(name, parts):
+            parts["small_" + name] = per_gate.tile([P, H], BF16, name="small_" + name)
+            transpose_eight([parts["rows_" + name][:, j, :] for j in range(H // P)], parts["small_" + name][:])
+
+        def start_tile(t):
+            position, half, m = where(t)
+            gate = GATE_ORDER[position]
             samples = slice(m * P, (m + 1) * P)
             units = slice(half * ROWS, (half + 1) * ROWS)
-            z = {}
+            parts = gate_parts[position]
+            weights = half_gate_weights[t // BATCH_TILES]
+            tile = {}
             for name in ("x", "h", "b"):
-                z[name] = psum_out.tile([P, ROWS], F32, name="z_" + name)
+                tile["z_" + name] = psum_out.tile([P, ROWS], F32, name="z_" + name)
                 nc.tensor.matmul(
-                    out=z[name][:], lhsT=emb_t[name][:, gate, samples], rhs=parts["small_" + name][:, units],
+                    out=tile["z_" + name][:], lhsT=emb_t[name][:, gate, samples], rhs=parts["small_" + name][:, units],
                     start=True, stop=True,
                 )
-            term = {}
-            for i, name in enumerate(("x", "h")):
-                product = psum_out.tile([P, ROWS], F32, name="product_" + name)
+            for name in ("x", "h"):
+                tile["z_sb_" + name] = z_pool.tile([P, ROWS], F32, name="z_sb_" + name)
+                nc.scalar.copy(out=tile["z_sb_" + name][:], in_=tile["z_" + name][:])
+                tile["product_" + name] = psum_out.tile([P, ROWS], F32, name="product_" + name)
                 for g in range(PASSES):
                     nc.tensor.matmul_mx(
-                        out=product[:],
+                        out=tile["product_" + name][:],
                         lhsT=act_codes[name][:, g, samples].bitcast(FP8X4),
                         lhsT_scale=act_scales[name][:, g, samples],
-                        rhs=parts["codes_" + name][:, g, units].bitcast(FP8X4),
-                        rhs_scale=parts["scales_" + name][:, g, units],
+                        rhs=weights["codes_" + name][:, g, :].bitcast(FP8X4),
+                        rhs_scale=weights["scales_" + name][:, g, :],
                         start=(g == 0),
                         stop=(g == PASSES - 1),
                     )
-                z_sb = work.tile([P, ROWS], F32, name="z_sb_" + name)
-                nc.scalar.copy(out=z_sb[:], in_=z[name][:])
-                term[name] = work.tile([P, ROWS], F32, name="term_" + name)
-                nc.vector.scalar_tensor_tensor(
-                    out=term[name][:], in0=product[:], scalar=1.0, in1=z_sb[:], op0=ALU.mult, op1=ALU.mult,
-                    accum_out=sums[:, 3 * half + i : 3 * half + i + 1],
-                )
-            term["b"] = work.tile([P, ROWS], F32, name="term_b")
-            nc.vector.scalar_tensor_tensor(
-                out=term["b"][:], in0=z["b"][:], scalar=1.0, in1=parts["bias"][:, units], op0=ALU.mult, op1=ALU.add,
-                accum_out=sums[:, 3 * half + 2 : 3 * half + 3],
-            )
-            nc.vector.tensor_tensor(out=term["x"][:], in0=term["x"][:], in1=term["h"][:], op=ALU.add)
-            nc.vector.tensor_tensor(out=pre[:, units], in0=term["x"][:], in1=term["b"][:], op=ALU.add)
+            return tile
 
-        def row_stats(values, sums):
-            total = stats.tile([P, 1], F32)
-            nc.vector.tensor_reduce(out=total[:], in_=sums, axis=AXIS.X, op=ALU.add)
+        def read_psum(t, tile):
+            position, half, m = where(t)
+            units = slice(half * ROWS, (half + 1) * ROWS)
+            for name in ("x", "h"):
+                tile["term_" + name] = work.tile([P, ROWS], F32, name="term_" + name)
+                nc.vector.tensor_tensor(
+                    out=tile["term_" + name][:], in0=tile["product_" + name][:], in1=tile["z_sb_" + name][:], op=ALU.mult,
+                )
+            tile["term_b"] = work.tile([P, ROWS], F32, name="term_b")
+            nc.vector.tensor_tensor(
+                out=tile["term_b"][:], in0=tile["z_b"][:], in1=gate_parts[position]["bias"][:, units], op=ALU.add,
+            )
+
+        def add_products(tile):
+            nc.vector.tensor_tensor(out=tile["term_x"][:], in0=tile["term_x"][:], in1=tile["term_h"][:], op=ALU.add)
+
+        def finish_tile(t, tile):
+            position, half, m = where(t)
+            units = slice(half * ROWS, (half + 1) * ROWS)
+            if half == 0:
+                rows[position, m] = {
+                    "pre": pre_pool.tile([P, H], F32, name="pre"),
+                    "sums": sums_pool.tile([P, HALVES], F32, name="sums"),
+                }
+            row = rows[position, m]
+            nc.vector.scalar_tensor_tensor(
+                out=row["pre"][:, units], in0=tile["term_x"][:], scalar=1.0, in1=tile["term_b"][:],
+                op0=ALU.mult, op1=ALU.add, accum_out=row["sums"][:, half : half + 1],
+            )
+
+        def start_stats(values, sums):
             neg_mean = stats.tile([P, 1], F32)
-            nc.vector.tensor_scalar_mul(out=neg_mean[:], in0=total[:], scalar1=-1.0 / H)
+            nc.gpsimd.tensor_scalar(
+                out=neg_mean[:], in0=sums[:, 0:1], scalar1=sums[:, 1:2], scalar2=-1.0 / H, op0=ALU.add, op1=ALU.mult,
+            )
             squares = scratch.tile([P, H], BF16)
             sum_sq = stats.tile([P, 1], F32)
             nc.scalar.activation(
@@ -171,91 +215,155 @@ def tile_hyperlstmcell_pb_kernel(
             root = stats.tile([P, 1], F32)
             nc.gpsimd.tensor_tensor(out=root[:], in0=sum_sq[:], in1=exp_half[:], op=ALU.pow)
             std_eps = stats.tile([P, 1], F32)
-            nc.vector.tensor_scalar(
+            nc.gpsimd.tensor_scalar(
                 out=std_eps[:], in0=root[:], scalar1=1.0 / math.sqrt(H - 1), scalar2=EPS, op0=ALU.mult, op1=ALU.add,
             )
             inv_std = stats.tile([P, 1], F32)
-            nc.vector.reciprocal(out=inv_std[:], in_=std_eps[:])
+            nc.gpsimd.tensor_tensor(out=inv_std[:], in0=std_eps[:], in1=exp_minus_one[:], op=ALU.pow)
             return neg_mean, inv_std
 
-        def normalise(out, values, neg_mean, inv_std, gain, shift):
+        def centre_and_gain(out, values, neg_mean, gain):
             nc.vector.scalar_tensor_tensor(
                 out=out, in0=values, scalar=neg_mean[:, 0:1], in1=gain, op0=ALU.add, op1=ALU.mult,
             )
+
+        def scale_and_shift(values, inv_std, shift):
             nc.vector.scalar_tensor_tensor(
-                out=out, in0=out, scalar=inv_std[:, 0:1], in1=shift, op0=ALU.mult, op1=ALU.add,
+                out=values, in0=values, scalar=inv_std[:, 0:1], in1=shift, op0=ALU.mult, op1=ALU.add,
             )
 
-        def finish_gate(gate, m, parts, pre, sums):
-            cell_m = cell[:, m, :]
-            neg_mean, inv_std = row_stats(pre[:], sums[:])
-            normalise(pre[:], pre[:], neg_mean, inv_std, parts["gain"][:], parts["shift"][:])
+        def activate(position, m):
+            gate, scaled = GATE_ORDER[position], rows[position, m]["scaled"]
             if gate == GATE_I:
-                nc.scalar.activation(out=cell_m, in_=pre[:], func=ACT.Sigmoid)
+                nc.scalar.activation(out=cell[:, m, :], in_=scaled[:], func=ACT.Sigmoid)
             elif gate == GATE_G:
-                nc.scalar.activation(out=pre[:], in_=pre[:], func=ACT.Tanh)
-                nc.vector.tensor_tensor(out=cell_m, in0=cell_m, in1=pre[:], op=ALU.mult)
-            elif gate == GATE_F:
-                nc.scalar.activation(out=pre[:], in_=pre[:], func=ACT.Sigmoid)
-                nc.vector.tensor_tensor(out=pre[:], in0=pre[:], in1=c_sb[:, m, :], op=ALU.mult)
-                cell_sum = stats.tile([P, 1], F32)
-                nc.vector.scalar_tensor_tensor(
-                    out=cell_m, in0=pre[:], scalar=1.0, in1=cell_m, op0=ALU.mult, op1=ALU.add, accum_out=cell_sum[:],
-                )
-                neg_mean, inv_std = row_stats(cell_m, cell_sum[:])
-                new_c = results.tile([P, H], F32, tag="result")
-                normalise(new_c[:], cell_m, neg_mean, inv_std, cell_gain[:], cell_shift[:])
-                nc.sync.dma_start(out=out_1[m * P : (m + 1) * P, :], in_=new_c[:])
-                nc.scalar.activation(out=cell_m, in_=new_c[:], func=ACT.Tanh)
+                nc.scalar.activation(out=scaled[:], in_=scaled[:], func=ACT.Tanh)
             else:
-                nc.scalar.activation(out=pre[:], in_=pre[:], func=ACT.Sigmoid)
+                nc.scalar.activation(out=scaled[:], in_=scaled[:], func=ACT.Sigmoid)
+
+        def use_gate(position, m):
+            gate, scaled = GATE_ORDER[position], rows[position, m]["scaled"]
+            if gate == GATE_G:
+                nc.vector.tensor_tensor(out=cell[:, m, :], in0=cell[:, m, :], in1=scaled[:], op=ALU.mult)
+            elif gate == GATE_F:
+                nc.vector.tensor_tensor(out=scaled[:], in0=scaled[:], in1=c_sb[:, m, :], op=ALU.mult)
+            elif gate == GATE_O:
                 new_h = results.tile([P, H], F32, tag="result")
-                nc.vector.tensor_tensor(out=new_h[:], in0=pre[:], in1=cell_m, op=ALU.mult)
+                nc.vector.tensor_tensor(out=new_h[:], in0=scaled[:], in1=cell[:, m, :], op=ALU.mult)
                 nc.sync.dma_start(out=out_0[m * P : (m + 1) * P, :], in_=new_h[:])
 
+        def add_cell(position, m):
+            row = rows[position, m]
+            cell_sums = sums_pool.tile([P, HALVES], F32)
+            for half in range(HALVES):
+                units = slice(half * ROWS, (half + 1) * ROWS)
+                nc.vector.scalar_tensor_tensor(
+                    out=cell[:, m, units], in0=row["scaled"][:, units], scalar=1.0, in1=cell[:, m, units],
+                    op0=ALU.mult, op1=ALU.add, accum_out=cell_sums[:, half : half + 1],
+                )
+            row["cell_neg_mean"], row["cell_inv_std"] = start_stats(cell[:, m, :], cell_sums)
+
+        gate_parts = {position: {} for position in range(GATES)}
+        load_gate_vectors(0, gate_parts[0])
+        act_rows = {"x": load_rows(x), "h": load_rows(h)}
+        emb_rows = {}
+        for name in ("x", "h", "b"):
+            emb_rows[name] = small_rows.tile([P, BATCH_TILES, GATES * E], BF16, name="emb_rows_" + name, tag="emb_rows")
+            nc.sync.dma_start(out=emb_rows[name][:], in_=embedding[name].rearrange("(m p) g e -> p m (g e)", p=P))
+        load_small_weights(0, gate_parts[0])
+
         act_codes, act_scales = {}, {}
-        for name, activations in (("x", x), ("h", h)):
+        for name in ("x", "h"):
             act_codes[name] = keep.tile([P, PASSES, B], U32, align_bytes=64, name="act_codes_" + name)
             act_scales[name] = keep.tile([P, PASSES, B], U8, align_bytes=64, name="act_scales_" + name)
-            rows_sb = load_rows(activations)
             for g in range(PASSES):
-                quantise_pass(rows_sb, g, act_codes[name][:, g, :], act_scales[name][:, g, :])
+                quantise(turn(act_rows[name], g, True), act_codes[name][:, g, :], act_scales[name][:, g, :])
 
         emb_t = {}
         for name in ("x", "h", "b"):
-            emb_rows = small_rows.tile([P, BATCH_TILES, GATES * E], BF16, tag="rows")
-            nc.sync.dma_start(out=emb_rows[:], in_=embedding[name].rearrange("(m p) g e -> p m (g e)", p=P))
             emb_t[name] = keep.tile([P, GATES, B], BF16, name="emb_t_" + name)
             for first_gate in range(0, GATES, 2):
                 transpose_eight(
                     [
-                        emb_rows[:, m, gate * E : (gate + 1) * E]
+                        emb_rows[name][:, m, gate * E : (gate + 1) * E]
                         for gate in (first_gate, first_gate + 1)
                         for m in range(BATCH_TILES)
                     ],
                     emb_t[name][:, first_gate : first_gate + 2, :].rearrange("p g b -> p (g b)"),
                 )
-
-        parts = {}
-        for step in range(STEPS):
-            prepare(GATE_ORDER[0], step, parts)
+            turn_small_weight(name, gate_parts[0])
 
         c_sb = keep.tile([P, BATCH_TILES, H], BF16)
-        nc.sync.dma_start(out=c_sb[:], in_=c.rearrange("(m p) n -> p m n", p=P))
         cell_gain = keep.tile([P, H], BF16)
-        nc.sync.dma_start(out=cell_gain[:], in_=lnc_gamma.partition_broadcast(P))
         cell_shift = keep.tile([P, H], BF16)
-        nc.sync.dma_start(out=cell_shift[:], in_=lnc_beta.partition_broadcast(P))
         cell = keep.tile([P, BATCH_TILES, H], F32)
 
-        for position, gate in enumerate(GATE_ORDER):
-            next_parts = {}
-            for m in range(BATCH_TILES):
-                pre = pre_pool.tile([P, H], F32)
-                sums = stats.tile([P, 3 * HALVES], F32)
-                for half in range(HALVES):
-                    output_tile(gate, m, half, parts, pre, sums)
-                    if position + 1 < GATES:
-                        prepare(GATE_ORDER[position + 1], m * HALVES + half, next_parts)
-                finish_gate(gate, m, parts, pre, sums)
-            parts = next_parts
+        step_rows, step_grouped, half_gate_weights, tiles, rows = {}, {}, {}, {}, {}
+        for t in range(-(TURN_AHEAD + LOAD_AHEAD), N_TILES + LAST_LAG):
+            has_tile = 0 <= t < N_TILES
+            row0, row1, row2, row3 = [completed_row(t - lag) for lag in range(LAST_LAG + 1)]
+            cell_row = row3 if row3 is not None and GATE_ORDER[row3[0]] == GATE_F else None
+
+            if has_tile:
+                read_psum(t, tiles[t])
+            if row1 is not None:
+                row = rows[row1]
+                row["scaled"] = scaled_pool.tile([P, H], F32, name="scaled")
+                centre_and_gain(row["scaled"][:], row["pre"][:], row["neg_mean"], gate_parts[row1[0]]["gain"][:])
+            if cell_row is not None:
+                new_c = results.tile([P, H], F32, tag="result")
+                centre_and_gain(new_c[:], cell[:, cell_row[1], :], rows[cell_row]["cell_neg_mean"], cell_gain[:])
+            if 0 <= t + 1 < N_TILES:
+                tiles[t + 1] = start_tile(t + 1)
+
+            q = t + TURN_AHEAD + LOAD_AHEAD
+            if 0 <= q < N_STEPS and q % PASSES == 0:
+                first_row = GATE_ORDER[q // (HALVES * STEPS_PER_HALF_GATE)] * H + (q // STEPS_PER_HALF_GATE) % HALVES * ROWS
+                matrix = big_weight[("x", "h")[(q % STEPS_PER_HALF_GATE) // PASSES]]
+                step_rows[q // PASSES] = load_rows(matrix[first_row : first_row + ROWS, :])
+            q = t + TURN_AHEAD
+            if 0 <= q < N_STEPS:
+                step_grouped[q] = turn(step_rows[q // PASSES], q % PASSES, t < 0)
+
+            if has_tile and t // TILES_PER_GATE + 1 < GATES:
+                next_position, slot_in_gate = t // TILES_PER_GATE + 1, t % TILES_PER_GATE
+                if slot_in_gate == 2:
+                    load_gate_vectors(next_position, gate_parts[next_position])
+                    load_small_weights(next_position, gate_parts[next_position])
+                if slot_in_gate in (4, 5, 6):
+                    turn_small_weight(("x", "h", "b")[slot_in_gate - 4], gate_parts[next_position])
+            if t == 0:
+                nc.sync.dma_start(out=c_sb[:], in_=c.rearrange("(m p) n -> p m n", p=P))
+                nc.gpsimd.dma_start(out=cell_gain[:], in_=lnc_gamma.partition_broadcast(P))
+                nc.gpsimd.dma_start(out=cell_shift[:], in_=lnc_beta.partition_broadcast(P))
+
+            if has_tile:
+                add_products(tiles[t])
+            q = t + QUANTISE_AHEAD
+            if 0 <= q < N_STEPS:
+                if q % STEPS_PER_HALF_GATE == 0:
+                    weights = {}
+                    for name in ("x", "h"):
+                        weights["codes_" + name] = half_gate.tile([P, PASSES, ROWS], U32, align_bytes=64, name="codes_" + name)
+                        weights["scales_" + name] = half_gate.tile([P, PASSES, ROWS], U8, align_bytes=64, name="scales_" + name)
+                    half_gate_weights[q // STEPS_PER_HALF_GATE] = weights
+                weights = half_gate_weights[q // STEPS_PER_HALF_GATE]
+                name, g = ("x", "h")[(q % STEPS_PER_HALF_GATE) // PASSES], q % PASSES
+                quantise(step_grouped[q], weights["codes_" + name][:, g, :], weights["scales_" + name][:, g, :])
+            if has_tile:
+                finish_tile(t, tiles[t])
+            if row0 is not None:
+                row = rows[row0]
+                row["neg_mean"], row["inv_std"] = start_stats(row["pre"][:], row["sums"])
+            if row2 is not None:
+                use_gate(row2[0], row2[1])
+            if row1 is not None:
+                scale_and_shift(rows[row1]["scaled"][:], rows[row1]["inv_std"], gate_parts[row1[0]]["shift"][:])
+                activate(row1[0], row1[1])
+            if row2 is not None and GATE_ORDER[row2[0]] == GATE_F:
+                add_cell(row2[0], row2[1])
+            if cell_row is not None:
+                m = cell_row[1]
+                scale_and_shift(new_c[:], rows[cell_row]["cell_inv_std"], cell_shift[:])
+                nc.sync.dma_start(out=out_1[m * P : (m + 1) * P, :], in_=new_c[:])
+                nc.scalar.activation(out=cell[:, m, :], in_=new_c[:], func=ACT.Tanh)

@@ -323,7 +323,7 @@ def tile_hyperlstmcell_pb_kernel(
                 step_rows[q // PASSES] = load_rows(matrix[first_row : first_row + ROWS, :])
             q = t + TURN_AHEAD
             if 0 <= q < N_STEPS:
-                step_grouped[q] = turn(step_rows[q // PASSES], q % PASSES, t < 0)
+                step_grouped[q] = turn(step_rows[q // PASSES], q % PASSES, True)
 
             if has_tile and t // TILES_PER_GATE + 1 < GATES:
                 next_position, slot_in_gate = t // TILES_PER_GATE + 1, t % TILES_PER_GATE

@@ -34,8 +34,9 @@ STEPS_PER_HALF_GATE = 2 * PASSES
 N_STEPS = GATES * HALVES * STEPS_PER_HALF_GATE
 QUANTISE_AHEAD = STEPS_PER_HALF_GATE + 1
 TURN_AHEAD = QUANTISE_AHEAD + 1
-LOAD_AHEAD = 6
-LAST_LAG = 3
+LOAD_AHEAD = 4
+LAST_LAG = 2
+UNIT_BLOCKS = H // P
 
 FLOPS = 2 * (2 * B * K * GATES * H) + 3 * (2 * B * E * GATES * H)
 
@@ -62,22 +63,23 @@ def tile_hyperlstmcell_pb_kernel(
     with ExitStack() as ctx:
         const = ctx.enter_context(tc.tile_pool(name="const", bufs=1))
         keep = ctx.enter_context(tc.tile_pool(name="keep", bufs=1))
-        big_rows = ctx.enter_context(tc.tile_pool(name="big_rows", bufs=4))
+        big_rows = ctx.enter_context(tc.tile_pool(name="big_rows", bufs=3))
         small_rows = ctx.enter_context(tc.tile_pool(name="small_rows", bufs=3))
         grouped_pool = ctx.enter_context(tc.tile_pool(name="grouped", bufs=3))
         half_gate = ctx.enter_context(tc.tile_pool(name="half_gate", bufs=2))
         per_gate = ctx.enter_context(tc.tile_pool(name="per_gate", bufs=2))
         work = ctx.enter_context(tc.tile_pool(name="work", bufs=2))
-        z_pool = ctx.enter_context(tc.tile_pool(name="z_sb", bufs=3))
-        pre_pool = ctx.enter_context(tc.tile_pool(name="pre", bufs=5))
+        z_pool = ctx.enter_context(tc.tile_pool(name="z_sb", bufs=2))
+        pre_pool = ctx.enter_context(tc.tile_pool(name="pre", bufs=8))
         sums_pool = ctx.enter_context(tc.tile_pool(name="sums", bufs=6))
-        scaled_pool = ctx.enter_context(tc.tile_pool(name="scaled", bufs=3))
+        scaled_pool = ctx.enter_context(tc.tile_pool(name="scaled", bufs=2))
+        block_pool = ctx.enter_context(tc.tile_pool(name="block", bufs=3))
+        cell_rows = ctx.enter_context(tc.tile_pool(name="cell_rows", bufs=BATCH_TILES))
         scratch = ctx.enter_context(tc.tile_pool(name="scratch", bufs=2))
         results = ctx.enter_context(tc.tile_pool(name="results", bufs=2))
         stats = ctx.enter_context(tc.tile_pool(name="stats", bufs=4))
         psum_out = ctx.enter_context(tc.psum_pool(name="psum_out", bufs=1))
         psum_turn = ctx.enter_context(tc.psum_pool(name="psum_turn", bufs=3))
-        ctx.enter_context(tc.manual_schedule())
 
         ident_f32 = const.tile([P, P], F32)
         make_identity(nc, ident_f32[:])
@@ -122,13 +124,10 @@ def tile_hyperlstmcell_pb_kernel(
                 nc.tensor.transpose(bank[:, i * P : (i + 1) * P], block, ident_bf16[:])
             nc.scalar.copy(out=dst, in_=bank[:])
 
-        def load_gate_vectors(position, parts):
+        def load_bias(position, parts):
             gate = GATE_ORDER[position]
-            for name, vector in (
-                ("bias", bias[gate * H : (gate + 1) * H]), ("gain", ln_gamma[gate, :]), ("shift", ln_beta[gate, :]),
-            ):
-                parts[name] = per_gate.tile([P, H], BF16, name=name)
-                nc.gpsimd.dma_start(out=parts[name][:], in_=vector.partition_broadcast(P))
+            parts["bias"] = per_gate.tile([P, H], BF16, name="bias")
+            nc.gpsimd.dma_start(out=parts["bias"][:], in_=bias[gate * H : (gate + 1) * H].partition_broadcast(P))
 
         def load_small_weights(position, parts):
             gate = GATE_ORDER[position]
@@ -232,45 +231,70 @@ def tile_hyperlstmcell_pb_kernel(
                 out=values, in0=values, scalar=inv_std[:, 0:1], in1=shift, op0=ALU.mult, op1=ALU.add,
             )
 
-        def activate(position, m):
-            gate, scaled = GATE_ORDER[position], rows[position, m]["scaled"]
+        def gate_block(position, j):
+            gate = GATE_ORDER[position]
+            block = slice(j * P, (j + 1) * P)
+            bank = psum_turn.tile([P, B], F32, tag="turned")
+            for m in range(BATCH_TILES):
+                nc.tensor.transpose(bank[:, m * P : (m + 1) * P], rows[position, m]["pre"][:, block], ident_f32[:])
+            column = gate * UNIT_BLOCKS + j
+            gain = unit_columns[:, column : column + 1]
+            shift = unit_columns[:, GATES * UNIT_BLOCKS + column : GATES * UNIT_BLOCKS + column + 1]
             if gate == GATE_I:
-                nc.scalar.activation(out=cell[:, m, :], in_=scaled[:], func=ACT.Sigmoid)
-            elif gate == GATE_G:
-                nc.scalar.activation(out=scaled[:], in_=scaled[:], func=ACT.Tanh)
-            else:
-                nc.scalar.activation(out=scaled[:], in_=scaled[:], func=ACT.Sigmoid)
-
-        def use_gate(position, m):
-            gate, scaled = GATE_ORDER[position], rows[position, m]["scaled"]
+                nc.scalar.activation(out=cell_t[:, j, :], in_=bank[:], func=ACT.Sigmoid, scale=gain, bias=shift)
+                return
+            activated = block_pool.tile([P, B], F32)
             if gate == GATE_G:
-                nc.vector.tensor_tensor(out=cell[:, m, :], in0=cell[:, m, :], in1=scaled[:], op=ALU.mult)
-            elif gate == GATE_F:
-                nc.vector.tensor_tensor(out=scaled[:], in0=scaled[:], in1=c_sb[:, m, :], op=ALU.mult)
-            elif gate == GATE_O:
-                new_h = results.tile([P, H], F32, tag="result")
-                nc.vector.tensor_tensor(out=new_h[:], in0=scaled[:], in1=cell[:, m, :], op=ALU.mult)
-                nc.sync.dma_start(out=out_0[m * P : (m + 1) * P, :], in_=new_h[:])
+                nc.scalar.activation(out=activated[:], in_=bank[:], func=ACT.Tanh, scale=gain, bias=shift)
+                nc.vector.tensor_tensor(out=cell_t[:, j, :], in0=cell_t[:, j, :], in1=activated[:], op=ALU.mult)
+            else:
+                nc.scalar.activation(out=activated[:], in_=bank[:], func=ACT.Sigmoid, scale=gain, bias=shift)
+                c_bank = psum_turn.tile([P, B], BF16, tag="turned")
+                for m in range(BATCH_TILES):
+                    nc.tensor.transpose(c_bank[:, m * P : (m + 1) * P], c_sb[:, m, block], ident_bf16[:])
+                nc.vector.tensor_tensor(out=activated[:], in0=c_bank[:], in1=activated[:], op=ALU.mult)
+                nc.vector.tensor_tensor(out=cell_t[:, j, :], in0=cell_t[:, j, :], in1=activated[:], op=ALU.add)
 
-        def add_cell(position, m):
-            row = rows[position, m]
-            cell_sums = sums_pool.tile([P, HALVES], F32)
+        def cell_back(m):
+            row = {
+                "values": cell_rows.tile([P, H], F32, name="cell_row"),
+                "sums": sums_pool.tile([P, HALVES], F32, name="cell_sums"),
+            }
             for half in range(HALVES):
-                units = slice(half * ROWS, (half + 1) * ROWS)
-                nc.vector.scalar_tensor_tensor(
-                    out=cell[:, m, units], in0=row["scaled"][:, units], scalar=1.0, in1=cell[:, m, units],
-                    op0=ALU.mult, op1=ALU.add, accum_out=cell_sums[:, half : half + 1],
+                bank = psum_turn.tile([P, ROWS], F32, tag="turned")
+                for i in range(ROWS // P):
+                    nc.tensor.transpose(
+                        bank[:, i * P : (i + 1) * P], cell_t[:, half * (ROWS // P) + i, m * P : (m + 1) * P], ident_f32[:],
+                    )
+                nc.scalar.activation(
+                    out=row["values"][:, half * ROWS : (half + 1) * ROWS], in_=bank[:], func=ACT.Identity,
+                    accum_out=row["sums"][:, half : half + 1],
                 )
-            row["cell_neg_mean"], row["cell_inv_std"] = start_stats(cell[:, m, :], cell_sums)
+            row["neg_mean"], row["inv_std"] = start_stats(row["values"][:], row["sums"])
+            return row
+
+        def finish_cell(m, row):
+            new_c = results.tile([P, H], F32, tag="result")
+            centre_and_gain(new_c[:], row["values"][:], row["neg_mean"], free_axis_vectors["gain_c"][:])
+            scale_and_shift(new_c[:], row["inv_std"], free_axis_vectors["shift_c"][:])
+            nc.sync.dma_start(out=out_1[m * P : (m + 1) * P, :], in_=new_c[:])
+            nc.scalar.activation(out=row["values"][:], in_=new_c[:], func=ACT.Tanh)
 
         gate_parts = {position: {} for position in range(GATES)}
-        load_gate_vectors(0, gate_parts[0])
+        load_bias(0, gate_parts[0])
         act_rows = {"x": load_rows(x), "h": load_rows(h)}
         emb_rows = {}
         for name in ("x", "h", "b"):
-            emb_rows[name] = small_rows.tile([P, BATCH_TILES, GATES * E], BF16, name="emb_rows_" + name, tag="emb_rows")
+            emb_rows[name] = pre_pool.tile([P, BATCH_TILES, GATES * E], BF16, name="emb_rows_" + name, tag="pre")
             nc.sync.dma_start(out=emb_rows[name][:], in_=embedding[name].rearrange("(m p) g e -> p m (g e)", p=P))
         load_small_weights(0, gate_parts[0])
+        vector_rows = const.tile([P, P], BF16)
+        nc.vector.memset(vector_rows[:], 0.0)
+        for first_row, vector in ((0, ln_gamma), (GATES * UNIT_BLOCKS, ln_beta)):
+            nc.sync.dma_start(
+                out=vector_rows[first_row : first_row + GATES * UNIT_BLOCKS, :],
+                in_=vector.rearrange("g (j p) -> (g j) p", p=P),
+            )
 
         act_codes, act_scales = {}, {}
         for name in ("x", "h"):
@@ -293,26 +317,26 @@ def tile_hyperlstmcell_pb_kernel(
                 )
             turn_small_weight(name, gate_parts[0])
 
-        c_sb = keep.tile([P, BATCH_TILES, H], BF16)
-        cell_gain = keep.tile([P, H], BF16)
-        cell_shift = keep.tile([P, H], BF16)
-        cell = keep.tile([P, BATCH_TILES, H], F32)
+        vector_bank = psum_turn.tile([P, P], BF16, tag="turned")
+        nc.tensor.transpose(vector_bank[:], vector_rows[:], ident_bf16[:])
+        unit_columns = const.tile([P, P], F32)
+        nc.scalar.copy(out=unit_columns[:], in_=vector_bank[:])
 
-        step_rows, step_grouped, half_gate_weights, tiles, rows = {}, {}, {}, {}, {}
+        c_sb = keep.tile([P, BATCH_TILES, H], BF16)
+        cell_t = keep.tile([P, UNIT_BLOCKS, B], F32)
+        free_axis_vectors = {}
+
+        step_rows, step_grouped, half_gate_weights, tiles, rows, cell_state = {}, {}, {}, {}, {}, {}
         for t in range(-(TURN_AHEAD + LOAD_AHEAD), N_TILES + LAST_LAG):
             has_tile = 0 <= t < N_TILES
-            row0, row1, row2, row3 = [completed_row(t - lag) for lag in range(LAST_LAG + 1)]
-            cell_row = row3 if row3 is not None and GATE_ORDER[row3[0]] == GATE_F else None
+            row0, row1, row2 = [completed_row(t - lag) for lag in range(LAST_LAG + 1)]
 
             if has_tile:
                 read_psum(t, tiles[t])
-            if row1 is not None:
+            if row1 is not None and GATE_ORDER[row1[0]] == GATE_O:
                 row = rows[row1]
                 row["scaled"] = scaled_pool.tile([P, H], F32, name="scaled")
-                centre_and_gain(row["scaled"][:], row["pre"][:], row["neg_mean"], gate_parts[row1[0]]["gain"][:])
-            if cell_row is not None:
-                new_c = results.tile([P, H], F32, tag="result")
-                centre_and_gain(new_c[:], cell[:, cell_row[1], :], rows[cell_row]["cell_neg_mean"], cell_gain[:])
+                centre_and_gain(row["scaled"][:], row["pre"][:], row["neg_mean"], free_axis_vectors["gain_o"][:])
             if 0 <= t + 1 < N_TILES:
                 tiles[t + 1] = start_tile(t + 1)
 
@@ -323,19 +347,23 @@ def tile_hyperlstmcell_pb_kernel(
                 step_rows[q // PASSES] = load_rows(matrix[first_row : first_row + ROWS, :])
             q = t + TURN_AHEAD
             if 0 <= q < N_STEPS:
-                step_grouped[q] = turn(step_rows[q // PASSES], q % PASSES, True)
+                step_grouped[q] = turn(step_rows[q // PASSES], q % PASSES, t < 0)
 
             if has_tile and t // TILES_PER_GATE + 1 < GATES:
                 next_position, slot_in_gate = t // TILES_PER_GATE + 1, t % TILES_PER_GATE
                 if slot_in_gate == 2:
-                    load_gate_vectors(next_position, gate_parts[next_position])
+                    load_bias(next_position, gate_parts[next_position])
                     load_small_weights(next_position, gate_parts[next_position])
                 if slot_in_gate in (4, 5, 6):
                     turn_small_weight(("x", "h", "b")[slot_in_gate - 4], gate_parts[next_position])
             if t == 0:
                 nc.sync.dma_start(out=c_sb[:], in_=c.rearrange("(m p) n -> p m n", p=P))
-                nc.gpsimd.dma_start(out=cell_gain[:], in_=lnc_gamma.partition_broadcast(P))
-                nc.gpsimd.dma_start(out=cell_shift[:], in_=lnc_beta.partition_broadcast(P))
+                for name, vector in (
+                    ("gain_c", lnc_gamma), ("shift_c", lnc_beta),
+                    ("gain_o", ln_gamma[GATE_O, :]), ("shift_o", ln_beta[GATE_O, :]),
+                ):
+                    free_axis_vectors[name] = keep.tile([P, H], BF16, name=name)
+                    nc.gpsimd.dma_start(out=free_axis_vectors[name][:], in_=vector.partition_broadcast(P))
 
             if has_tile:
                 add_products(tiles[t])
@@ -352,18 +380,36 @@ def tile_hyperlstmcell_pb_kernel(
                 quantise(step_grouped[q], weights["codes_" + name][:, g, :], weights["scales_" + name][:, g, :])
             if has_tile:
                 finish_tile(t, tiles[t])
+
             if row0 is not None:
                 row = rows[row0]
                 row["neg_mean"], row["inv_std"] = start_stats(row["pre"][:], row["sums"])
-            if row2 is not None:
-                use_gate(row2[0], row2[1])
+            if row2 is not None and GATE_ORDER[row2[0]] == GATE_O:
+                m = row2[1]
+                new_h = results.tile([P, H], F32, tag="result")
+                nc.vector.tensor_tensor(out=new_h[:], in0=rows[row2]["scaled"][:], in1=cell_state[m]["values"][:], op=ALU.mult)
+                nc.sync.dma_start(out=out_0[m * P : (m + 1) * P, :], in_=new_h[:])
             if row1 is not None:
-                scale_and_shift(rows[row1]["scaled"][:], rows[row1]["inv_std"], gate_parts[row1[0]]["shift"][:])
-                activate(row1[0], row1[1])
-            if row2 is not None and GATE_ORDER[row2[0]] == GATE_F:
-                add_cell(row2[0], row2[1])
-            if cell_row is not None:
-                m = cell_row[1]
-                scale_and_shift(new_c[:], rows[cell_row]["cell_inv_std"], cell_shift[:])
-                nc.sync.dma_start(out=out_1[m * P : (m + 1) * P, :], in_=new_c[:])
-                nc.scalar.activation(out=cell[:, m, :], in_=new_c[:], func=ACT.Tanh)
+                row = rows[row1]
+                if GATE_ORDER[row1[0]] == GATE_O:
+                    scale_and_shift(row["scaled"][:], row["inv_std"], free_axis_vectors["shift_o"][:])
+                    nc.scalar.activation(out=row["scaled"][:], in_=row["scaled"][:], func=ACT.Sigmoid)
+                else:
+                    offset = stats.tile([P, 1], F32)
+                    nc.gpsimd.tensor_tensor(out=offset[:], in0=row["neg_mean"][:], in1=row["inv_std"][:], op=ALU.mult)
+                    nc.scalar.activation(
+                        out=row["pre"][:], in_=row["pre"][:], func=ACT.Identity, scale=row["inv_std"][:, 0:1], bias=offset[:, 0:1],
+                    )
+
+            if has_tile and t >= TILES_PER_GATE:
+                previous, slot_in_gate = t // TILES_PER_GATE - 1, t % TILES_PER_GATE
+                if slot_in_gate in (1, 2):
+                    for j in range((slot_in_gate - 1) * UNIT_BLOCKS // 2, slot_in_gate * UNIT_BLOCKS // 2):
+                        gate_block(previous, j)
+                if GATE_ORDER[previous] == GATE_F:
+                    if slot_in_gate in (4, 5):
+                        for m in range((slot_in_gate - 4) * BATCH_TILES // 2, (slot_in_gate - 3) * BATCH_TILES // 2):
+                            finish_cell(m, cell_state[m])
+                    if slot_in_gate in (3, 4):
+                        for m in range((slot_in_gate - 3) * BATCH_TILES // 2, (slot_in_gate - 2) * BATCH_TILES // 2):
+                            cell_state[m] = cell_back(m)

@@ -37,6 +37,10 @@ TURN_AHEAD = QUANTISE_AHEAD + 1
 LOAD_AHEAD = 4
 LAST_LAG = 2
 UNIT_BLOCKS = H // P
+VECTOR_HELPS_UNTIL = 2 * TILES_PER_GATE
+BLOCKS_PER_SLOT = 2
+FIRST_BACK_SLOT = 1 + UNIT_BLOCKS // BLOCKS_PER_SLOT
+BACK_PER_SLOT = 2
 
 FLOPS = 2 * (2 * B * K * GATES * H) + 3 * (2 * B * E * GATES * H)
 
@@ -347,15 +351,15 @@ def tile_hyperlstmcell_pb_kernel(
                 step_rows[q // PASSES] = load_rows(matrix[first_row : first_row + ROWS, :])
             q = t + TURN_AHEAD
             if 0 <= q < N_STEPS:
-                step_grouped[q] = turn(step_rows[q // PASSES], q % PASSES, t < 0)
+                step_grouped[q] = turn(step_rows[q // PASSES], q % PASSES, t < VECTOR_HELPS_UNTIL)
 
             if has_tile and t // TILES_PER_GATE + 1 < GATES:
                 next_position, slot_in_gate = t // TILES_PER_GATE + 1, t % TILES_PER_GATE
-                if slot_in_gate == 2:
+                if slot_in_gate == 0:
                     load_bias(next_position, gate_parts[next_position])
                     load_small_weights(next_position, gate_parts[next_position])
-                if slot_in_gate in (4, 5, 6):
-                    turn_small_weight(("x", "h", "b")[slot_in_gate - 4], gate_parts[next_position])
+                if slot_in_gate in (1, 2, 3):
+                    turn_small_weight(("x", "h", "b")[slot_in_gate - 1], gate_parts[next_position])
             if t == 0:
                 nc.sync.dma_start(out=c_sb[:], in_=c.rearrange("(m p) n -> p m n", p=P))
                 for name, vector in (
@@ -384,11 +388,6 @@ def tile_hyperlstmcell_pb_kernel(
             if row0 is not None:
                 row = rows[row0]
                 row["neg_mean"], row["inv_std"] = start_stats(row["pre"][:], row["sums"])
-            if row2 is not None and GATE_ORDER[row2[0]] == GATE_O:
-                m = row2[1]
-                new_h = results.tile([P, H], F32, tag="result")
-                nc.vector.tensor_tensor(out=new_h[:], in0=rows[row2]["scaled"][:], in1=cell_state[m]["values"][:], op=ALU.mult)
-                nc.sync.dma_start(out=out_0[m * P : (m + 1) * P, :], in_=new_h[:])
             if row1 is not None:
                 row = rows[row1]
                 if GATE_ORDER[row1[0]] == GATE_O:
@@ -403,13 +402,21 @@ def tile_hyperlstmcell_pb_kernel(
 
             if has_tile and t >= TILES_PER_GATE:
                 previous, slot_in_gate = t // TILES_PER_GATE - 1, t % TILES_PER_GATE
-                if slot_in_gate in (1, 2):
-                    for j in range((slot_in_gate - 1) * UNIT_BLOCKS // 2, slot_in_gate * UNIT_BLOCKS // 2):
+                if 1 <= slot_in_gate < FIRST_BACK_SLOT:
+                    for j in range((slot_in_gate - 1) * BLOCKS_PER_SLOT, slot_in_gate * BLOCKS_PER_SLOT):
                         gate_block(previous, j)
                 if GATE_ORDER[previous] == GATE_F:
-                    if slot_in_gate in (4, 5):
-                        for m in range((slot_in_gate - 4) * BATCH_TILES // 2, (slot_in_gate - 3) * BATCH_TILES // 2):
+                    first = (slot_in_gate - FIRST_BACK_SLOT - 1) * BACK_PER_SLOT
+                    if 0 <= first < BATCH_TILES:
+                        for m in range(first, first + BACK_PER_SLOT):
                             finish_cell(m, cell_state[m])
-                    if slot_in_gate in (3, 4):
-                        for m in range((slot_in_gate - 3) * BATCH_TILES // 2, (slot_in_gate - 2) * BATCH_TILES // 2):
+                    first = (slot_in_gate - FIRST_BACK_SLOT) * BACK_PER_SLOT
+                    if 0 <= first < BATCH_TILES:
+                        for m in range(first, first + BACK_PER_SLOT):
                             cell_state[m] = cell_back(m)
+
+            if row2 is not None and GATE_ORDER[row2[0]] == GATE_O:
+                m = row2[1]
+                new_h = results.tile([P, H], F32, tag="result")
+                nc.vector.tensor_tensor(out=new_h[:], in0=rows[row2]["scaled"][:], in1=cell_state[m]["values"][:], op=ALU.mult)
+                nc.sync.dma_start(out=out_0[m * P : (m + 1) * P, :], in_=new_h[:])

@@ -29,6 +29,7 @@ EPS = 1e-6
 
 GATE_I, GATE_F, GATE_G, GATE_O = 0, 1, 2, 3
 GATE_ORDER = (GATE_I, GATE_G, GATE_F, GATE_O)
+FIRST_BIAS_ROW_GATE = 1
 
 STEPS_PER_HALF_GATE = 2 * PASSES
 N_STEPS = GATES * HALVES * STEPS_PER_HALF_GATE
@@ -128,11 +129,6 @@ def tile_hyperlstmcell_pb_kernel(
                 nc.tensor.transpose(bank[:, i * P : (i + 1) * P], block, ident_bf16[:])
             nc.scalar.copy(out=dst, in_=bank[:])
 
-        def load_bias(position, parts):
-            gate = GATE_ORDER[position]
-            parts["bias"] = per_gate.tile([P, H], BF16, name="bias")
-            nc.gpsimd.dma_start(out=parts["bias"][:], in_=bias[gate * H : (gate + 1) * H].partition_broadcast(P))
-
         def load_small_weights(position, parts):
             gate = GATE_ORDER[position]
             for name in ("x", "h", "b"):
@@ -153,7 +149,7 @@ def tile_hyperlstmcell_pb_kernel(
             parts = gate_parts[position]
             weights = half_gate_weights[t // BATCH_TILES]
             tile = {}
-            for name in ("x", "h", "b"):
+            for name in ("x", "h"):
                 tile["z_" + name] = psum_out.tile([P, ROWS], F32, name="z_" + name)
                 nc.tensor.matmul(
                     out=tile["z_" + name][:], lhsT=emb_t[name][:, gate, samples], rhs=parts["small_" + name][:, units],
@@ -175,18 +171,27 @@ def tile_hyperlstmcell_pb_kernel(
                     )
             return tile
 
-        def read_psum(t, tile):
+        def start_offset(t, tile):
             position, half, m = where(t)
+            gate = GATE_ORDER[position]
             units = slice(half * ROWS, (half + 1) * ROWS)
+            tile["z_b"] = psum_out.tile([P, ROWS], F32, name="z_b")
+            nc.tensor.matmul(
+                out=tile["z_b"][:], lhsT=emb_t["b"][:, gate, m * P : (m + 1) * P], rhs=gate_parts[position]["small_b"][:, units],
+                start=True, stop=(position == 0),
+            )
+            if position > 0:
+                first_unit = (gate - FIRST_BIAS_ROW_GATE) * H + half * ROWS
+                nc.tensor.matmul(
+                    out=tile["z_b"][:], lhsT=ones[:], rhs=bias_rows[:, first_unit : first_unit + ROWS], start=False, stop=True,
+                )
+
+        def read_psum(t, tile):
             for name in ("x", "h"):
                 tile["term_" + name] = work.tile([P, ROWS], F32, name="term_" + name)
                 nc.vector.tensor_tensor(
                     out=tile["term_" + name][:], in0=tile["product_" + name][:], in1=tile["z_sb_" + name][:], op=ALU.mult,
                 )
-            tile["term_b"] = work.tile([P, ROWS], F32, name="term_b")
-            nc.vector.tensor_tensor(
-                out=tile["term_b"][:], in0=tile["z_b"][:], in1=gate_parts[position]["bias"][:, units], op=ALU.add,
-            )
 
         def add_products(tile):
             nc.vector.tensor_tensor(out=tile["term_x"][:], in0=tile["term_x"][:], in1=tile["term_h"][:], op=ALU.add)
@@ -200,8 +205,10 @@ def tile_hyperlstmcell_pb_kernel(
                     "sums": sums_pool.tile([P, HALVES], F32, name="sums"),
                 }
             row = rows[position, m]
+            if position == 0:
+                nc.vector.tensor_tensor(out=tile["term_x"][:], in0=tile["term_x"][:], in1=first_bias[:, units], op=ALU.add)
             nc.vector.scalar_tensor_tensor(
-                out=row["pre"][:, units], in0=tile["term_x"][:], scalar=1.0, in1=tile["term_b"][:],
+                out=row["pre"][:, units], in0=tile["z_b"][:], scalar=1.0, in1=tile["term_x"][:],
                 op0=ALU.mult, op1=ALU.add, accum_out=row["sums"][:, half : half + 1],
             )
 
@@ -285,7 +292,13 @@ def tile_hyperlstmcell_pb_kernel(
             nc.scalar.activation(out=row["values"][:], in_=new_c[:], func=ACT.Tanh)
 
         gate_parts = {position: {} for position in range(GATES)}
-        load_bias(0, gate_parts[0])
+        first_bias = keep.tile([P, H], BF16)
+        nc.gpsimd.dma_start(out=first_bias[:], in_=bias[GATE_ORDER[0] * H : (GATE_ORDER[0] + 1) * H].partition_broadcast(P))
+        ones = const.tile([P, P], BF16)
+        nc.vector.memset(ones[:], 1.0)
+        bias_rows = keep.tile([P, (GATES - FIRST_BIAS_ROW_GATE) * H], BF16)
+        nc.vector.memset(bias_rows[:], 0.0)
+        nc.sync.dma_start(out=bias_rows[0:1, :], in_=bias[FIRST_BIAS_ROW_GATE * H :].unsqueeze(0))
         act_rows = {"x": load_rows(x), "h": load_rows(h)}
         emb_rows = {}
         for name in ("x", "h", "b"):
@@ -356,7 +369,6 @@ def tile_hyperlstmcell_pb_kernel(
             if has_tile and t // TILES_PER_GATE + 1 < GATES:
                 next_position, slot_in_gate = t // TILES_PER_GATE + 1, t % TILES_PER_GATE
                 if slot_in_gate == 0:
-                    load_bias(next_position, gate_parts[next_position])
                     load_small_weights(next_position, gate_parts[next_position])
                 if slot_in_gate in (1, 2, 3):
                     turn_small_weight(("x", "h", "b")[slot_in_gate - 1], gate_parts[next_position])
@@ -384,6 +396,8 @@ def tile_hyperlstmcell_pb_kernel(
                 quantise(step_grouped[q], weights["codes_" + name][:, g, :], weights["scales_" + name][:, g, :])
             if has_tile:
                 finish_tile(t, tiles[t])
+            if 0 <= t + 1 < N_TILES:
+                start_offset(t + 1, tiles[t + 1])
 
             if row0 is not None:
                 row = rows[row0]

import math
from contextlib import ExitStack

import concourse.mybir as mybir
from concourse.masks import make_identity

F32 = mybir.dt.float32
BF16 = mybir.dt.bfloat16
U32 = mybir.dt.uint32
U8 = mybir.dt.uint8
FP8X4 = mybir.dt.float8_e4m3fn_x4
ACT = mybir.ActivationFunctionType
ALU = mybir.AluOpType

P = 128
B = 512
K = 1024
H = 1024
E = 128
GATES = 4
BATCH_TILES = B // P
K_PASS = 4 * P
PASSES = K // K_PASS
ROWS = 512
HALVES = H // ROWS
TILES_PER_GATE = HALVES * BATCH_TILES
N_TILES = GATES * TILES_PER_GATE
EPS = 1e-6

GATE_I, GATE_F, GATE_G, GATE_O = 0, 1, 2, 3
GATE_ORDER = (GATE_I, GATE_G, GATE_F, GATE_O)
FIRST_BIAS_ROW_GATE = 1

STEPS_PER_HALF_GATE = 2 * PASSES
N_STEPS = GATES * HALVES * STEPS_PER_HALF_GATE
QUANTISE_AHEAD = STEPS_PER_HALF_GATE + 1
TURN_AHEAD = QUANTISE_AHEAD + 1
LOAD_AHEAD = 4
LAST_LAG = 2
UNIT_BLOCKS = H // P
VECTOR_HELPS_UNTIL = 2 * TILES_PER_GATE
BLOCKS_PER_SLOT = 2
FIRST_BACK_SLOT = 1 + UNIT_BLOCKS // BLOCKS_PER_SLOT
BACK_PER_SLOT = 2

FLOPS = 2 * (2 * B * K * GATES * H) + 3 * (2 * B * E * GATES * H)


def where(t):
    return t // TILES_PER_GATE, (t % TILES_PER_GATE) // BATCH_TILES, t % BATCH_TILES


def completed_row(t):
    if 0 <= t < N_TILES and where(t)[1] == HALVES - 1:
        return where(t)[0], where(t)[2]
    return None


def tile_hyperlstmcell_pb_kernel(
    tc, x, h, c, emb_h, emb_x, emb_b, Wsh, Wsx, Wsb, Wih, Whh, bias,
    ln_gamma, ln_beta, lnc_gamma, lnc_beta, out_0, out_1,
):
    nc = tc.nc
    big_weight = {"x": Wih, "h": Whh}
    small_weight = {"x": Wsx, "h": Wsh, "b": Wsb}
    embedding = {"x": emb_x, "h": emb_h, "b": emb_b}

    with ExitStack() as ctx:
        const = ctx.enter_context(tc.tile_pool(name="const", bufs=1))
        keep = ctx.enter_context(tc.tile_pool(name="keep", bufs=1))
        big_rows = ctx.enter_context(tc.tile_pool(name="big_rows", bufs=3))
        small_rows = ctx.enter_context(tc.tile_pool(name="small_rows", bufs=3))
        grouped_pool = ctx.enter_context(tc.tile_pool(name="grouped", bufs=3))
        half_gate = ctx.enter_context(tc.tile_pool(name="half_gate", bufs=2))
        per_gate = ctx.enter_context(tc.tile_pool(name="per_gate", bufs=2))
        work = ctx.enter_context(tc.tile_pool(name="work", bufs=2))
        z_pool = ctx.enter_context(tc.tile_pool(name="z_sb", bufs=2))
        pre_pool = ctx.enter_context(tc.tile_pool(name="pre", bufs=8))
        sums_pool = ctx.enter_context(tc.tile_pool(name="sums", bufs=6))
        scaled_pool = ctx.enter_context(tc.tile_pool(name="scaled", bufs=2))
        block_pool = ctx.enter_context(tc.tile_pool(name="block", bufs=3))
        cell_rows = ctx.enter_context(tc.tile_pool(name="cell_rows", bufs=BATCH_TILES))
        scratch = ctx.enter_context(tc.tile_pool(name="scratch", bufs=2))
        results = ctx.enter_context(tc.tile_pool(name="results", bufs=2))
        stats = ctx.enter_context(tc.tile_pool(name="stats", bufs=4))
        psum_out = ctx.enter_context(tc.psum_pool(name="psum_out", bufs=1))
        psum_turn = ctx.enter_context(tc.psum_pool(name="psum_turn", bufs=3))

        ident_f32 = const.tile([P, P], F32)
        make_identity(nc, ident_f32[:])
        ident_bf16 = const.tile([P, P], BF16)
        make_identity(nc, ident_bf16[:])
        exp_half = const.tile([P, 1], F32)
        nc.vector.memset(exp_half[:], 0.5)
        exp_minus_one = const.tile([P, 1], F32)
        nc.vector.memset(exp_minus_one[:], -1.0)

        def load_rows(dram_rows):
            rows_sb = big_rows.tile([P, ROWS // P, K], BF16)
            nc.sync.dma_start(out=rows_sb[:], in_=dram_rows.rearrange("(r p) k -> p r k", p=P))
            return rows_sb

        def turn(rows_sb, g, vector_helps):
            grouped = grouped_pool.tile([P, 4 * ROWS], BF16, align_bytes=64)
            grouped_words = grouped[:].bitcast(F32).rearrange("p (r u) -> p r u", u=2)
            for pair in range(2):
                bank = psum_turn.tile([P, 2, 2 * P], F32, tag="turned")
                for u in range(2):
                    for r in range(2):
                        first_word = 2 * P * g + P * u
                        nc.tensor.transpose(
                            bank[:, u, r * P : (r + 1) * P],
                            rows_sb[:, 2 * pair + r, :].bitcast(F32)[:, first_word : first_word + P],
                            ident_f32[:],
                        )
                target = grouped_words[:, 2 * P * pair : 2 * P * (pair + 1), :]
                if vector_helps and pair == 1:
                    nc.vector.tensor_copy(out=target, in_=bank[:].rearrange("p u r -> p r u"))
                else:
                    nc.scalar.copy(out=target, in_=bank[:].rearrange("p u r -> p r u"))
            return grouped

        def quantise(grouped, codes, scales):
            nc.vector.quantize_mx(out=codes.bitcast(FP8X4), scales=scales, in_=grouped[:])

        def transpose_eight(blocks, dst):
            bank = psum_turn.tile([P, 8 * P], BF16, tag="turned")
            for i, block in enumerate(blocks):
                nc.tensor.transpose(bank[:, i * P : (i + 1) * P], block, ident_bf16[:])
            nc.scalar.copy(out=dst, in_=bank[:])

        def load_small_weights(position, parts):
            gate = GATE_ORDER[position]
            for name in ("x", "h", "b"):
                parts["rows_" + name] = small_rows.tile([P, H // P, E], BF16, name="rows_" + name, tag="rows")
                nc.sync.dma_start(
                    out=parts["rows_" + name][:], in_=small_weight[name][gate].rearrange("(j p) e -> p j e", p=P)
                )

        def turn_small_weight(name, parts):
            parts["small_" + name] = per_gate.tile([P, H], BF16, name="small_" + name)
            transpose_eight([parts["rows_" + name][:, j, :] for j in range(H // P)], parts["small_" + name][:])

        def start_tile(t):
            position, half, m = where(t)
            gate = GATE_ORDER[position]
            samples = slice(m * P, (m + 1) * P)
            units = slice(half * ROWS, (half + 1) * ROWS)
            parts = gate_parts[position]
            weights = half_gate_weights[t // BATCH_TILES]
            tile = {}
            for name in ("x", "h"):
                tile["z_" + name] = psum_out.tile([P, ROWS], F32, name="z_" + name)
                nc.tensor.matmul(
                    out=tile["z_" + name][:], lhsT=emb_t[name][:, gate, samples], rhs=parts["small_" + name][:, units],
                    start=True, stop=True,
                )
            for name in ("x", "h"):
                tile["z_sb_" + name] = z_pool.tile([P, ROWS], F32, name="z_sb_" + name)
                nc.scalar.copy(out=tile["z_sb_" + name][:], in_=tile["z_" + name][:])
                tile["product_" + name] = psum_out.tile([P, ROWS], F32, name="product_" + name)
                for g in range(PASSES):
                    nc.tensor.matmul_mx(
                        out=tile["product_" + name][:],
                        lhsT=act_codes[name][:, g, samples].bitcast(FP8X4),
                        lhsT_scale=act_scales[name][:, g, samples],
                        rhs=weights["codes_" + name][:, g, :].bitcast(FP8X4),
                        rhs_scale=weights["scales_" + name][:, g, :],
                        start=(g == 0),
                        stop=(g == PASSES - 1),
                    )
            return tile

        def start_offset(t, tile):
            position, half, m = where(t)
            gate = GATE_ORDER[position]
            units = slice(half * ROWS, (half + 1) * ROWS)
            tile["z_b"] = psum_out.tile([P, ROWS], F32, name="z_b")
            nc.tensor.matmul(
                out=tile["z_b"][:], lhsT=emb_t["b"][:, gate, m * P : (m + 1) * P], rhs=gate_parts[position]["small_b"][:, units],
                start=True, stop=(position == 0),
            )
            if position > 0:
                first_unit = (gate - FIRST_BIAS_ROW_GATE) * H + half * ROWS
                nc.tensor.matmul(
                    out=tile["z_b"][:], lhsT=ones[:], rhs=bias_rows[:, first_unit : first_unit + ROWS], start=False, stop=True,
                )

        def read_psum(t, tile):
            for name in ("x", "h"):
                tile["term_" + name] = work.tile([P, ROWS], F32, name="term_" + name)
                nc.vector.tensor_tensor(
                    out=tile["term_" + name][:], in0=tile["product_" + name][:], in1=tile["z_sb_" + name][:], op=ALU.mult,
                )

        def add_products(tile):
            nc.vector.tensor_tensor(out=tile["term_x"][:], in0=tile["term_x"][:], in1=tile["term_h"][:], op=ALU.add)

        def finish_tile(t, tile):
            position, half, m = where(t)
            units = slice(half * ROWS, (half + 1) * ROWS)
            if half == 0:
                rows[position, m] = {
                    "pre": pre_pool.tile([P, H], F32, name="pre"),
                    "sums": sums_pool.tile([P, HALVES], F32, name="sums"),
                }
            row = rows[position, m]
            if position == 0:
                nc.vector.tensor_tensor(out=tile["term_x"][:], in0=tile["term_x"][:], in1=first_bias[:, units], op=ALU.add)
            nc.vector.scalar_tensor_tensor(
                out=row["pre"][:, units], in0=tile["z_b"][:], scalar=1.0, in1=tile["term_x"][:],
                op0=ALU.mult, op1=ALU.add, accum_out=row["sums"][:, half : half + 1],
            )

        def start_stats(values, sums):
            neg_mean = stats.tile([P, 1], F32)
            nc.gpsimd.tensor_scalar(
                out=neg_mean[:], in0=sums[:, 0:1], scalar1=sums[:, 1:2], scalar2=-1.0 / H, op0=ALU.add, op1=ALU.mult,
            )
            squares = scratch.tile([P, H], BF16)
            sum_sq = stats.tile([P, 1], F32)
            nc.scalar.activation(
                out=squares[:], in_=values, func=ACT.Square, bias=neg_mean[:, 0:1], scale=1.0, accum_out=sum_sq[:],
            )
            root = stats.tile([P, 1], F32)
            nc.gpsimd.tensor_tensor(out=root[:], in0=sum_sq[:], in1=exp_half[:], op=ALU.pow)
            std_eps = stats.tile([P, 1], F32)
            nc.gpsimd.tensor_scalar(
                out=std_eps[:], in0=root[:], scalar1=1.0 / math.sqrt(H - 1), scalar2=EPS, op0=ALU.mult, op1=ALU.add,
            )
            inv_std = stats.tile([P, 1], F32)
            nc.gpsimd.tensor_tensor(out=inv_std[:], in0=std_eps[:], in1=exp_minus_one[:], op=ALU.pow)
            return neg_mean, inv_std

        def centre_and_gain(out, values, neg_mean, gain):
            nc.vector.scalar_tensor_tensor(
                out=out, in0=values, scalar=neg_mean[:, 0:1], in1=gain, op0=ALU.add, op1=ALU.mult,
            )

        def scale_and_shift(values, inv_std, shift):
            nc.vector.scalar_tensor_tensor(
                out=values, in0=values, scalar=inv_std[:, 0:1], in1=shift, op0=ALU.mult, op1=ALU.add,
            )

        def gate_block(position, j):
            gate = GATE_ORDER[position]
            block = slice(j * P, (j + 1) * P)
            bank = psum_turn.tile([P, B], F32, tag="turned")
            for m in range(BATCH_TILES):
                nc.tensor.transpose(bank[:, m * P : (m + 1) * P], rows[position, m]["pre"][:, block], ident_f32[:])
            column = gate * UNIT_BLOCKS + j
            gain = unit_columns[:, column : column + 1]
            shift = unit_columns[:, GATES * UNIT_BLOCKS + column : GATES * UNIT_BLOCKS + column + 1]
            if gate == GATE_I:
                nc.scalar.activation(out=cell_t[:, j, :], in_=bank[:], func=ACT.Sigmoid, scale=gain, bias=shift)
                return
            activated = block_pool.tile([P, B], F32)
            if gate == GATE_G:
                nc.scalar.activation(out=activated[:], in_=bank[:], func=ACT.Tanh, scale=gain, bias=shift)
                nc.vector.tensor_tensor(out=cell_t[:, j, :], in0=cell_t[:, j, :], in1=activated[:], op=ALU.mult)
            else:
                nc.scalar.activation(out=activated[:], in_=bank[:], func=ACT.Sigmoid, scale=gain, bias=shift)
                c_bank = psum_turn.tile([P, B], BF16, tag="turned")
                for m in range(BATCH_TILES):
                    nc.tensor.transpose(c_bank[:, m * P : (m + 1) * P], c_sb[:, m, block], ident_bf16[:])
                nc.vector.tensor_tensor(out=activated[:], in0=c_bank[:], in1=activated[:], op=ALU.mult)
                nc.vector.tensor_tensor(out=cell_t[:, j, :], in0=cell_t[:, j, :], in1=activated[:], op=ALU.add)

        def cell_back(m):
            row = {
                "values": cell_rows.tile([P, H], F32, name="cell_row"),
                "sums": sums_pool.tile([P, HALVES], F32, name="cell_sums"),
            }
            for half in range(HALVES):
                bank = psum_turn.tile([P, ROWS], F32, tag="turned")
                for i in range(ROWS // P):
                    nc.tensor.transpose(
                        bank[:, i * P : (i + 1) * P], cell_t[:, half * (ROWS // P) + i, m * P : (m + 1) * P], ident_f32[:],
                    )
                nc.scalar.activation(
                    out=row["values"][:, half * ROWS : (half + 1) * ROWS], in_=bank[:], func=ACT.Identity,
                    accum_out=row["sums"][:, half : half + 1],
                )
            row["neg_mean"], row["inv_std"] = start_stats(row["values"][:], row["sums"])
            return row

        def finish_cell(m, row):
            new_c = results.tile([P, H], F32, tag="result")
            centre_and_gain(new_c[:], row["values"][:], row["neg_mean"], free_axis_vectors["gain_c"][:])
            scale_and_shift(new_c[:], row["inv_std"], free_axis_vectors["shift_c"][:])
            nc.sync.dma_start(out=out_1[m * P : (m + 1) * P, :], in_=new_c[:])
            nc.scalar.activation(out=row["values"][:], in_=new_c[:], func=ACT.Tanh)

        gate_parts = {position: {} for position in range(GATES)}
        first_bias = keep.tile([P, H], BF16)
        nc.gpsimd.dma_start(out=first_bias[:], in_=bias[GATE_ORDER[0] * H : (GATE_ORDER[0] + 1) * H].partition_broadcast(P))
        ones = const.tile([P, P], BF16)
        nc.vector.memset(ones[:], 1.0)
        bias_rows = keep.tile([P, (GATES - FIRST_BIAS_ROW_GATE) * H], BF16)
        nc.vector.memset(bias_rows[:], 0.0)
        nc.sync.dma_start(out=bias_rows[0:1, :], in_=bias[FIRST_BIAS_ROW_GATE * H :].unsqueeze(0))
        act_rows = {"x": load_rows(x), "h": load_rows(h)}
        emb_rows = {}
        for name in ("x", "h", "b"):
            emb_rows[name] = pre_pool.tile([P, BATCH_TILES, GATES * E], BF16, name="emb_rows_" + name, tag="pre")
            nc.sync.dma_start(out=emb_rows[name][:], in_=embedding[name].rearrange("(m p) g e -> p m (g e)", p=P))
        load_small_weights(0, gate_parts[0])
        vector_rows = const.tile([P, P], BF16)
        nc.vector.memset(vector_rows[:], 0.0)
        for first_row, vector in ((0, ln_gamma), (GATES * UNIT_BLOCKS, ln_beta)):
            nc.sync.dma_start(
                out=vector_rows[first_row : first_row + GATES * UNIT_BLOCKS, :],
                in_=vector.rearrange("g (j p) -> (g j) p", p=P),
            )

        act_codes, act_scales = {}, {}
        for name in ("x", "h"):
            act_codes[name] = keep.tile([P, PASSES, B], U32, align_bytes=64, name="act_codes_" + name)
            act_scales[name] = keep.tile([P, PASSES, B], U8, align_bytes=64, name="act_scales_" + name)
            for g in range(PASSES):
                quantise(turn(act_rows[name], g, True), act_codes[name][:, g, :], act_scales[name][:, g, :])

        emb_t = {}
        for name in ("x", "h", "b"):
            emb_t[name] = keep.tile([P, GATES, B], BF16, name="emb_t_" + name)
            for first_gate in range(0, GATES, 2):
                transpose_eight(
                    [
                        emb_rows[name][:, m, gate * E : (gate + 1) * E]
                        for gate in (first_gate, first_gate + 1)
                        for m in range(BATCH_TILES)
                    ],
                    emb_t[name][:, first_gate : first_gate + 2, :].rearrange("p g b -> p (g b)"),
                )
            turn_small_weight(name, gate_parts[0])

        vector_bank = psum_turn.tile([P, P], BF16, tag="turned")
        nc.tensor.transpose(vector_bank[:], vector_rows[:], ident_bf16[:])
        unit_columns = const.tile([P, P], F32)
        nc.scalar.copy(out=unit_columns[:], in_=vector_bank[:])

        c_sb = keep.tile([P, BATCH_TILES, H], BF16)
        cell_t = keep.tile([P, UNIT_BLOCKS, B], F32)
        free_axis_vectors = {}

        step_rows, step_grouped, half_gate_weights, tiles, rows, cell_state = {}, {}, {}, {}, {}, {}
        for t in range(-(TURN_AHEAD + LOAD_AHEAD), N_TILES + LAST_LAG):
            has_tile = 0 <= t < N_TILES
            row0, row1, row2 = [completed_row(t - lag) for lag in range(LAST_LAG + 1)]

            if has_tile:
                read_psum(t, tiles[t])
            if row1 is not None and GATE_ORDER[row1[0]] == GATE_O:
                row = rows[row1]
                row["scaled"] = scaled_pool.tile([P, H], F32, name="scaled")
                centre_and_gain(row["scaled"][:], row["pre"][:], row["neg_mean"], free_axis_vectors["gain_o"][:])
            if 0 <= t + 1 < N_TILES:
                tiles[t + 1] = start_tile(t + 1)

            q = t + TURN_AHEAD + LOAD_AHEAD
            if 0 <= q < N_STEPS and q % PASSES == 0:
                first_row = GATE_ORDER[q // (HALVES * STEPS_PER_HALF_GATE)] * H + (q // STEPS_PER_HALF_GATE) % HALVES * ROWS
                matrix = big_weight[("x", "h")[(q % STEPS_PER_HALF_GATE) // PASSES]]
                step_rows[q // PASSES] = load_rows(matrix[first_row : first_row + ROWS, :])
            q = t + TURN_AHEAD
            if 0 <= q < N_STEPS:
                step_grouped[q] = turn(step_rows[q // PASSES], q % PASSES, t < VECTOR_HELPS_UNTIL)

            if has_tile and t // TILES_PER_GATE + 1 < GATES:
                next_position, slot_in_gate = t // TILES_PER_GATE + 1, t % TILES_PER_GATE
                if slot_in_gate == 0:
                    load_small_weights(next_position, gate_parts[next_position])
                if slot_in_gate in (1, 2, 3):
                    turn_small_weight(("x", "h", "b")[slot_in_gate - 1], gate_parts[next_position])
            if t == 0:
                nc.sync.dma_start(out=c_sb[:], in_=c.rearrange("(m p) n -> p m n", p=P))
                for name, vector in (
                    ("gain_c", lnc_gamma), ("shift_c", lnc_beta),
                    ("gain_o", ln_gamma[GATE_O, :]), ("shift_o", ln_beta[GATE_O, :]),
                ):
                    free_axis_vectors[name] = keep.tile([P, H], BF16, name=name)
                    nc.gpsimd.dma_start(out=free_axis_vectors[name][:], in_=vector.partition_broadcast(P))

            if has_tile:
                add_products(tiles[t])
            q = t + QUANTISE_AHEAD
            if 0 <= q < N_STEPS:
                if q % STEPS_PER_HALF_GATE == 0:
                    weights = {}
                    for name in ("x", "h"):
                        weights["codes_" + name] = half_gate.tile([P, PASSES, ROWS], U32, align_bytes=64, name="codes_" + name)
                        weights["scales_" + name] = half_gate.tile([P, PASSES, ROWS], U8, align_bytes=64, name="scales_" + name)
                    half_gate_weights[q // STEPS_PER_HALF_GATE] = weights
                weights = half_gate_weights[q // STEPS_PER_HALF_GATE]
                name, g = ("x", "h")[(q % STEPS_PER_HALF_GATE) // PASSES], q % PASSES
                quantise(step_grouped[q], weights["codes_" + name][:, g, :], weights["scales_" + name][:, g, :])
            if has_tile:
                finish_tile(t, tiles[t])
            if 0 <= t + 1 < N_TILES:
                start_offset(t + 1, tiles[t + 1])

            if row0 is not None:
                row = rows[row0]
                row["neg_mean"], row["inv_std"] = start_stats(row["pre"][:], row["sums"])
            if row1 is not None:
                row = rows[row1]
                if GATE_ORDER[row1[0]] == GATE_O:
                    scale_and_shift(row["scaled"][:], row["inv_std"], free_axis_vectors["shift_o"][:])
                    nc.scalar.activation(out=row["scaled"][:], in_=row["scaled"][:], func=ACT.Sigmoid)
                else:
                    offset = stats.tile([P, 1], F32)
                    nc.gpsimd.tensor_tensor(out=offset[:], in0=row["neg_mean"][:], in1=row["inv_std"][:], op=ALU.mult)
                    nc.scalar.activation(
                        out=row["pre"][:], in_=row["pre"][:], func=ACT.Identity, scale=row["inv_std"][:, 0:1], bias=offset[:, 0:1],
                    )

            if has_tile and t >= TILES_PER_GATE:
                previous, slot_in_gate = t // TILES_PER_GATE - 1, t % TILES_PER_GATE
                if 1 <= slot_in_gate < FIRST_BACK_SLOT:
                    for j in range((slot_in_gate - 1) * BLOCKS_PER_SLOT, slot_in_gate * BLOCKS_PER_SLOT):
                        gate_block(previous, j)
                if GATE_ORDER[previous] == GATE_F:
                    first = (slot_in_gate - FIRST_BACK_SLOT - 1) * BACK_PER_SLOT
                    if 0 <= first < BATCH_TILES:
                        for m in range(first, first + BACK_PER_SLOT):
                            finish_cell(m, cell_state[m])
                    first = (slot_in_gate - FIRST_BACK_SLOT) * BACK_PER_SLOT
                    if 0 <= first < BATCH_TILES:
                        for m in range(first, first + BACK_PER_SLOT):
                            cell_state[m] = cell_back(m)

            if row2 is not None and GATE_ORDER[row2[0]] == GATE_O:
                m = row2[1]
                new_h = results.tile([P, H], F32, tag="result")
                nc.vector.tensor_tensor(out=new_h[:], in0=rows[row2]["scaled"][:], in1=cell_state[m]["values"][:], op=ALU.mult)
                nc.sync.dma_start(out=out_0[m * P : (m + 1) * P, :], in_=new_h[:])
